import numpy as np
import ml_dtypes


def mxq(x, axis, fmt="e4m3"):
    dtype, down = {"e4m3": (ml_dtypes.float8_e4m3fn, 7), "e5m2": (ml_dtypes.float8_e5m2, 14)}[fmt]
    v = np.moveaxis(np.asarray(x, np.float32).astype(ml_dtypes.bfloat16).astype(np.float64), axis, -1)
    blocks = v.reshape(v.shape[:-1] + (-1, 32))
    amax = np.abs(blocks).max(-1, keepdims=True)
    byte = np.maximum(np.where(amax > 0, np.frexp(amax)[1] - 1 + 127, 0) - down, 1)
    scale = np.exp2(byte - 127.0)
    codes = (blocks / scale).astype(np.float32).astype(dtype).astype(np.float64)
    return np.moveaxis((codes * scale).reshape(v.shape), -1, axis)


WIDE = False


def mx_kscale(k):
    if not WIDE:
        return np.ones(k)
    levels = np.array([10, -10, 5, -5, 0])
    if k % 512:
        return np.exp2(np.random.permutation(np.resize(levels, k // 32))).repeat(32)
    a = np.empty((k // 512, 16))
    for p in range(k // 512):
        a[p, :8] = np.random.permutation(np.resize(levels, 8))
        for g in range(8):
            far = levels[np.abs(levels - a[p, g]) >= 10]
            a[p, g + 8] = far[np.random.randint(len(far))]
    return np.exp2(a.ravel()).repeat(32)


BF16 = ml_dtypes.bfloat16


def bf(x):
    return np.asarray(x, np.float32).astype(BF16)


def f64(x):
    return np.asarray(x).astype(np.float64)


B, H, W, C, NH, WS, SH, HID = 2, 48, 48, 1024, 16, 16, 7, 512
HD = C // NH
WW = WS * WS
PT, PL = WS - SH, WS - SH
HP, WP = H + WS, W + WS
NWH, NWW = HP // WS, WP // WS
NWIN = B * NWH * NWW
EPS = 1e-5
ERF_CLIP, ERF_TERMS = 6.0, 100


def erf(z):
    z = np.clip(z, -ERF_CLIP, ERF_CLIP)
    zz = 2.0 * z * z
    term = z.copy()
    total = z.copy()
    for n in range(1, ERF_TERMS):
        term = term * zz / (2.0 * n + 1.0)
        total = total + term
    return 2.0 / np.sqrt(np.pi) * np.exp(-z * z) * total


def gelu(v):
    return 0.5 * v * (1.0 + erf(v / np.sqrt(2.0)))


def layer_norm(x, g, b):
    m = x.mean(-1, keepdims=True)
    v = ((x - m) ** 2).mean(-1, keepdims=True)
    return (x - m) / np.sqrt(v + EPS) * g + b


def setup_inputs():
    r = np.random.standard_normal
    s = mx_kscale(C)
    return {
        "h_pad": bf(r((B, HP, WP, C)) * 0.7),
        "x": bf(r((B, H * W, C))),
        "sw": bf(r((NH, WW, WW)) / np.sqrt(WW)),
        "sb": bf(r((NH, WW)) * 0.3),
        "g2": bf((1.0 + 0.2 * r(C)) * s),
        "b2": bf(0.2 * r(C) * s),
        "w1": bf(r((C, HID)) / np.sqrt(C) / s[:, None]),
        "bb1": bf(r(HID) * 0.3),
    }


def reference(h_pad, x, sw, sb, g2, b2, w1, bb1):
    hw = (f64(h_pad).reshape(B, NWH, WS, NWW, WS, NH, HD)
          .transpose(5, 2, 4, 0, 1, 3, 6)
          .reshape(NH, WW, NWIN * HD))
    m = f64(sw) @ hw + f64(sb)[:, :, None]
    m = (m.reshape(NH, WS, WS, B, NWH, NWW, HD)
          .transpose(3, 4, 1, 5, 2, 0, 6)
          .reshape(B, HP, WP, C))
    m = m[:, PT:PT + H, PL:PL + W, :].reshape(B, H * W, C)
    x1 = f64(x) + m
    h2 = layer_norm(x1, f64(g2), f64(b2))
    a = (mxq(h2, 2, "e4m3") @ mxq(f64(w1), 0, "e4m3")) + f64(bb1)
    return gelu(a)

@@ -1,0 +1,429 @@
+from contextlib import ExitStack
+
+import concourse.mybir as mybir
+from concourse.masks import make_identity
+
+F32 = mybir.dt.float32
+BF16 = mybir.dt.bfloat16
+I32 = mybir.dt.int32
+U32 = mybir.dt.uint32
+U8 = mybir.dt.uint8
+FP8X4 = mybir.dt.float8_e4m3fn_x4
+ALU = mybir.AluOpType
+ACT = mybir.ActivationFunctionType
+
+P = 128
+IMAGES = 2
+WS = 16
+WINDOWS = 4
+CROP = 9
+MAP = 48
+C = 1024
+HEADS = 16
+HD = C // HEADS
+HID = 512
+EPS = 1e-5
+ROWS = 8
+SEAM = CROP + MAP - WS * (WINDOWS - 1)
+LEFT = SEAM * ROWS
+UNITS = 6
+PACK = 4
+K_PASS = P * PACK
+PASSES = C // K_PASS
+BLOCKS = C // P
+STRIP = ROWS * MAP
+STRIP_TILES = STRIP // P
+MARGIN = 16
+SPLIT = LEFT + P
+
+FLOPS = 2 * HEADS * (WS * WS) * (WS * WS) * (IMAGES * WINDOWS * WINDOWS * HD) + 2 * IMAGES * MAP * MAP * C * HID
+
+
+def tile_swinmlpblock_pa_t_kernel(tc, h_pad, x, sw, sb, g2, b2, w1, bb1, out):
+    nc = tc.nc
+    with ExitStack() as ctx:
+        const = ctx.enter_context(tc.tile_pool(name="const", bufs=1))
+        win_pool = ctx.enter_context(tc.tile_pool(name="windows", bufs=2))
+        x_pool = ctx.enter_context(tc.tile_pool(name="x", bufs=2))
+        x1_pool = ctx.enter_context(tc.tile_pool(name="x1", bufs=2))
+        small = ctx.enter_context(tc.tile_pool(name="small", bufs=3))
+        spare_pool = ctx.enter_context(tc.tile_pool(name="spare", bufs=1))
+        plane_pool = ctx.enter_context(tc.tile_pool(name="planes", bufs=2))
+        group_pool = ctx.enter_context(tc.tile_pool(name="grouped", bufs=2))
+        code_pool = ctx.enter_context(tc.tile_pool(name="codes", bufs=2))
+        act_pool = ctx.enter_context(tc.tile_pool(name="act", bufs=3))
+        psum = ctx.enter_context(tc.psum_pool(name="psum", bufs=8))
+
+        win_view = h_pad.rearrange("b (wr r) (wc k q) c -> b wr wc r k (q c)", r=WS, wc=WINDOWS, k=WS // 2, q=2)
+        x_view = x.rearrange("b (y w) c -> b w y c", w=MAP)
+
+        ident_f = const.tile([P, P], F32)
+        make_identity(nc, ident_f[:])
+        ident_b = const.tile([P, P], BF16)
+        make_identity(nc, ident_b[:])
+        by_rows = const.tile([P, ROWS, WS], F32)
+        nc.vector.tensor_copy(out=by_rows[:], in_=ident_f[:].rearrange("p (c r) -> p r c", c=WS, r=ROWS))
+        minus_half = const.tile([P, 2], F32)
+        nc.vector.memset(minus_half[:], -0.5)
+
+        def load_windows(wrow):
+            inner = win_pool.tile([P, 4, 2, C], BF16, tag="inner")
+            last = win_pool.tile([P, 2, 2, C], BF16, tag="last")
+            first = win_pool.tile([P, 2, 2, C], BF16, tag="first")
+            for b in range(IMAGES):
+                for wcol in (1, 2):
+                    nc.sync.dma_start(
+                        out=inner[:, 2 * b + wcol - 1, :, :].rearrange("p q c -> p (q c)"),
+                        in_=win_view[b, wrow, wcol],
+                    )
+            for b in range(IMAGES):
+                nc.sync.dma_start(
+                    out=last[:, b, :, :].rearrange("p q c -> p (q c)"), in_=win_view[b, wrow, WINDOWS - 1]
+                )
+                nc.sync.dma_start(out=first[:, b, :, :].rearrange("p q c -> p (q c)"), in_=win_view[b, wrow, 0])
+            return inner, last, first
+
+        def load_x(y0, y_last):
+            x_sb = x_pool.tile([P, UNITS, C], BF16, tag="x")
+            for b in range(IMAGES):
+                pieces = [(0, P, 2 * b + wcol - 1, WS * wcol - CROP) for wcol in (1, 2)]
+                pieces.append((0, LEFT, 4 + b, MAP - SEAM))
+                pieces.append((LEFT, P, 4 + b, 0))
+                for p0, p1, n, w0 in pieces:
+                    w1_ = w0 + (p1 - p0) // ROWS
+                    nc.sync.dma_start(out=x_sb[p0:p1, n, :], in_=x_view[b, w0:w1_, y0 : y0 + ROWS, :])
+                    if y_last != y0 + ROWS - 1:
+                        nc.sync.dma_start(out=x_sb[p0 + ROWS - 1 : p1 : ROWS, n, :], in_=x_view[b, w0:w1_, y_last, :])
+            return x_sb
+
+        sw_nat = x1_pool.tile([P, 2, HEADS, WS * WS], BF16, tag="x1")
+        sw_view = sw.rearrange("h (t p) j -> t p h j", t=2)
+        nc.sync.dma_start(out=sw_nat[:, 0], in_=sw_view[0])
+        windows = load_windows(1)
+        x_next = load_x(WS - CROP, WS - CROP + ROWS - 1)
+        nc.sync.dma_start(out=sw_nat[:, 1], in_=sw_view[1])
+
+        vec_rows = act_pool.tile([P, K_PASS], BF16, tag="act")
+        nc.vector.memset(vec_rows[:].bitcast(I32), 0)
+        nc.scalar.dma_start(out=vec_rows[0:PASSES, :], in_=g2.rearrange("(g c) -> g c", c=K_PASS))
+        nc.scalar.dma_start(out=vec_rows[PASSES : 2 * PASSES, :], in_=b2.rearrange("(g c) -> g c", c=K_PASS))
+        vec_perm = act_pool.tile([P, PACK, P], BF16, tag="act")
+        nc.vector.tensor_copy(out=vec_perm[:], in_=vec_rows[:].rearrange("p (q t) -> p t q", t=PACK))
+        sb_rows = act_pool.tile([P, 2 * P], BF16, tag="act")
+        nc.vector.memset(sb_rows[:].bitcast(I32), 0)
+        nc.scalar.dma_start(out=sb_rows[0:HEADS, :], in_=sb)
+        bias_bc = const.tile([P, HID], BF16)
+        nc.scalar.dma_start(out=bias_bc[:], in_=bb1.partition_broadcast(P))
+        sb_perm = act_pool.tile([P, 3, WS, ROWS], BF16, tag="act")
+        nc.vector.tensor_copy(
+            out=sb_perm[:, 0:2, :, :], in_=sb_rows[:].rearrange("p (t r c) -> p t c r", t=2, r=ROWS, c=WS)
+        )
+        nc.vector.tensor_copy(out=sb_perm[:, 2, :, 0 : ROWS - 1], in_=sb_perm[:, 1, :, 1:ROWS])
+        nc.vector.tensor_copy(out=sb_perm[:, 2, :, ROWS - 1 : ROWS], in_=sb_perm[:, 1, :, 0:1])
+        vec_ps = psum.tile([P, PACK + 3, P], BF16, tag="bank")
+        for t in range(PACK):
+            nc.tensor.transpose(out=vec_ps[:, t, :], in_=vec_perm[:, t, :], identity=ident_b[:])
+        for i in range(3):
+            nc.tensor.transpose(
+                out=vec_ps[:, PACK + i, :], in_=sb_perm[:, i, :, :].rearrange("p c r -> p (c r)"), identity=ident_b[:]
+            )
+        gain_shift = const.tile([P, 2 * BLOCKS], F32)
+        nc.vector.tensor_copy(
+            out=gain_shift[:].rearrange("p (r t) -> p r t", t=PACK),
+            in_=vec_ps[:, 0:PACK, 0 : 2 * PASSES].rearrange("p t r -> p r t"),
+        )
+        sb_col = const.tile([P, 3, HEADS], F32)
+        nc.vector.tensor_copy(out=sb_col[:], in_=vec_ps[:, PACK : PACK + 3, 0:HEADS])
+
+        n_blocks = 2 * HEADS
+        whole = [const.tile([P, 2 * MARGIN + n_blocks * P], BF16, name="whole%d" % half) for half in range(2)]
+        split = [const.tile([P, 2 * MARGIN + n_blocks * SPLIT], BF16, name="split%d" % half) for half in range(2)]
+        orphan = const.tile([P, 2 * MARGIN + n_blocks * SPLIT], BF16)
+        for t in whole:
+            nc.vector.memset(t[:, 0:MARGIN].bitcast(I32), 0)
+            nc.vector.memset(t[:, MARGIN + n_blocks * P :].bitcast(I32), 0)
+        for t in split + [orphan]:
+            nc.vector.memset(t[:].bitcast(I32), 0)
+
+        def by_block(t, width):
+            return t[:, MARGIN : MARGIN + n_blocks * width].rearrange("p (n m) -> p n m", m=width)
+
+        def prepare_weights(half):
+            for quad in range(HEADS // 4):
+                sw_ps = psum.tile([P, 8, P], BF16, tag="bank")
+                for i in range(8):
+                    h, q = 4 * quad + i // 2, i % 2
+                    nc.tensor.transpose(
+                        out=sw_ps[:, i, :],
+                        in_=sw_nat[:, half, h, :].rearrange("p (k q) -> p q k", q=2)[:, q, :],
+                        identity=ident_b[:],
+                    )
+                dst = by_block(whole[half], P)[:, 8 * quad : 8 * (quad + 1), :].rearrange(
+                    "p n (c r) -> p n c r", c=WS, r=ROWS
+                )
+                src = sw_ps[:].rearrange("p n (r c) -> p n c r", r=ROWS, c=WS)
+                if quad % 2 == 0:
+                    nc.vector.tensor_copy(out=dst, in_=src)
+                else:
+                    nc.scalar.copy(out=dst, in_=src)
+            nc.vector.tensor_copy(out=by_block(split[half], SPLIT)[:, :, 0:LEFT], in_=by_block(whole[half], P)[:, :, 0:LEFT])
+            nc.vector.tensor_copy(
+                out=by_block(split[half], SPLIT)[:, :, 2 * LEFT : SPLIT], in_=by_block(whole[half], P)[:, :, LEFT:P]
+            )
+
+        def first_rows(t, width, m0, m1):
+            return by_block(t, width)[:, :, m0:m1].rearrange("p n (c r) -> p n c r", r=ROWS)[:, :, :, 0:1]
+
+        def prepare_seam_weights():
+            nc.gpsimd.tensor_copy(out=first_rows(orphan, SPLIT, 0, LEFT), in_=first_rows(split[1], SPLIT, 0, LEFT))
+            nc.gpsimd.tensor_copy(
+                out=first_rows(orphan, SPLIT, 2 * LEFT, SPLIT), in_=first_rows(split[1], SPLIT, 2 * LEFT, SPLIT)
+            )
+            nc.gpsimd.memset(first_rows(whole[1], P, 0, P), 0.0)
+            nc.gpsimd.memset(first_rows(split[1], SPLIT, 0, LEFT), 0.0)
+            nc.gpsimd.memset(first_rows(split[1], SPLIT, 2 * LEFT, SPLIT), 0.0)
+
+        prepare_weights(0)
+
+        w1_codes = const.tile([P, PASSES, HID], U32, align_bytes=64)
+        w1_scales = const.tile([P, PASSES, HID], U8, align_bytes=64)
+
+        def prepare_w1():
+            w1_view = w1.rearrange("(g p t) n -> g p t n", g=PASSES, t=PACK)
+            for g in range(PASSES):
+                raw = plane_pool.tile([P, PACK, HID], BF16, tag="planes")
+                nc.sync.dma_start(out=raw[:], in_=w1_view[g])
+                grouped = group_pool.tile([P, HID, PACK], BF16, tag="grouped", align_bytes=64)
+                nc.vector.tensor_copy(out=grouped[:], in_=raw[:].rearrange("p t n -> p n t"))
+                nc.vector.quantize_mx(
+                    out=w1_codes[:, g, :].bitcast(FP8X4),
+                    scales=w1_scales[:, g, :],
+                    in_=grouped[:].rearrange("p n t -> p (n t)"),
+                )
+
+        def accumulate(acc, terms):
+            for i, (weights, moving) in enumerate(terms):
+                nc.tensor.matmul(out=acc, lhsT=weights, rhs=moving, start=(i == 0), stop=(i == len(terms) - 1))
+
+        def mix(sources, sb_index, x_sb, x1, heads):
+            for h in heads:
+                cols = slice(HD * h, HD * (h + 1))
+                inner_terms, seam_terms = [], []
+                for (inner, last, first), whole_w, split_w, start in sources:
+                    for q in range(2):
+                        n = 2 * h + q
+                        s0 = MARGIN + SPLIT * n + start
+                        left_w = split_w[:, s0 : s0 + P]
+                        right_w = split_w[:, s0 + LEFT : s0 + LEFT + P]
+                        if whole_w is None:
+                            inner_terms.append((left_w, inner[:, :, q, cols]))
+                            inner_terms.append((right_w, inner[:, :, q, cols]))
+                        else:
+                            w0 = MARGIN + P * n + start
+                            inner_terms.append((whole_w[:, w0 : w0 + P], inner[:, :, q, cols]))
+                        seam_terms.append((left_w, last[:, :, q, cols]))
+                        seam_terms.append((right_w, first[:, :, q, cols]))
+                acc = psum.tile([P, UNITS, HD], F32, tag="bank")
+                accumulate(acc[:, 0:4, :], inner_terms)
+                accumulate(acc[:, 4:6, :], seam_terms)
+                nc.vector.scalar_tensor_tensor(
+                    out=x1[:, :, cols],
+                    in0=acc[:],
+                    scalar=sb_col[:, sb_index, h : h + 1],
+                    in1=x_sb[:, :, cols],
+                    op0=ALU.add,
+                    op1=ALU.add,
+                )
+
+        def statistics(x1, x_sb, b):
+            seam, inner = 4 + b, (2 * b, 2 * b + 1)
+            stats = small.tile([P, 2, 6], F32, tag="stats")
+            for i in range(2):
+                nc.vector.bn_stats(out=stats[:, i, :], in_=x1[:, seam, 512 * i : 512 * (i + 1)])
+            mean_var = small.tile([P, 2], F32, tag="mean_var")
+            nc.vector.bn_aggr(out=mean_var[:], in_=stats[:])
+            sums = small.tile([P, 2], F32, tag="sums")
+            for j, n in enumerate(inner):
+                nc.scalar.activation(out=x_sb[:, n, :], in_=x1[:, n, :], func=ACT.Identity, accum_out=sums[:, j : j + 1])
+            neg_mean = small.tile([P, 2], F32, tag="neg_mean")
+            nc.scalar.mul(out=neg_mean[:], in_=sums[:], mul=-1.0 / C)
+            squares = small.tile([P, 2], F32, tag="squares")
+            for j, n in enumerate(inner):
+                nc.scalar.activation(
+                    out=x_sb[:, n, :],
+                    in_=x1[:, n, :],
+                    func=ACT.Square,
+                    bias=neg_mean[:, j : j + 1],
+                    accum_out=squares[:, j : j + 1],
+                )
+            return mean_var, neg_mean, squares
+
+        def slots(x1, spare, b):
+            if b == 0:
+                return spare[:], x1[:, 4, :], x1[:, 0, :]
+            return x1[:, 1, :], x1[:, 5, :], x1[:, 2, :]
+
+        def permuted(slot):
+            return slot.rearrange("p (g t q) -> p g q t", g=PASSES, t=PACK)
+
+        def scale(x1, spare, b, mean_var, neg_mean, squares):
+            seam, inner = 4 + b, (2 * b, 2 * b + 1)
+            to = slots(x1, spare, b)
+            seam_scalars = small.tile([P, 2], F32, tag="seam_scalars")
+            nc.gpsimd.tensor_scalar(
+                out=seam_scalars[:, 0:1], in0=mean_var[:, 0:1], scalar1=-1.0, scalar2=0.0, op0=ALU.mult, op1=ALU.add
+            )
+            nc.gpsimd.tensor_scalar(
+                out=seam_scalars[:, 1:2], in0=mean_var[:, 1:2], scalar1=1.0, scalar2=EPS, op0=ALU.mult, op1=ALU.add
+            )
+            nc.gpsimd.tensor_tensor(
+                out=seam_scalars[:, 1:2], in0=seam_scalars[:, 1:2], in1=minus_half[:, 0:1], op=ALU.pow
+            )
+            rstd = small.tile([P, 2], F32, tag="rstd")
+            nc.gpsimd.tensor_scalar(
+                out=rstd[:], in0=squares[:], scalar1=1.0 / C, scalar2=EPS, op0=ALU.mult, op1=ALU.add
+            )
+            nc.gpsimd.tensor_tensor(out=rstd[:], in0=rstd[:], in1=minus_half[:], op=ALU.pow)
+            nc.vector.tensor_scalar(
+                out=permuted(to[0]),
+                in0=x1[:, seam, :].rearrange("p (g q t) -> p g q t", g=PASSES, t=PACK),
+                scalar1=seam_scalars[:, 0:1],
+                scalar2=seam_scalars[:, 1:2],
+                op0=ALU.add,
+                op1=ALU.mult,
+            )
+            for j, n in enumerate(inner):
+                nc.vector.tensor_scalar(
+                    out=permuted(to[1 + j]),
+                    in0=x1[:, n, :].rearrange("p (g q t) -> p g q t", g=PASSES, t=PACK),
+                    scalar1=neg_mean[:, j : j + 1],
+                    scalar2=rstd[:, j : j + 1],
+                    op0=ALU.add,
+                    op1=ALU.mult,
+                )
+
+        def flip(x1, spare, b):
+            planes = plane_pool.tile([P, BLOCKS, 3 * P], BF16, tag="planes")
+            for k in range(BLOCKS):
+                turned = psum.tile([P, ROWS, MAP], F32, tag="bank")
+                for slot, y in enumerate(slots(x1, spare, b)):
+                    nc.tensor.transpose(
+                        out=turned[:, :, WS * slot : WS * (slot + 1)],
+                        in_=y[:, P * k : P * (k + 1)],
+                        identity=by_rows[:],
+                    )
+                nc.scalar.activation(
+                    out=planes[:, k, :],
+                    in_=turned[:].rearrange("p r w -> p (r w)"),
+                    func=ACT.Identity,
+                    scale=gain_shift[:, k : k + 1],
+                    bias=gain_shift[:, BLOCKS + k : BLOCKS + k + 1],
+                )
+            return planes
+
+        def pack(planes):
+            grouped = group_pool.tile([P, PASSES, STRIP, PACK], BF16, tag="grouped", align_bytes=64)
+            codes = code_pool.tile([P, PASSES, STRIP], U32, tag="codes", align_bytes=64)
+            scales = code_pool.tile([P, PASSES, STRIP], U8, tag="scales", align_bytes=64)
+            for g in range(PASSES):
+                src = planes[:, PACK * g : PACK * (g + 1), :].rearrange("p t (r w) -> p r w t", r=ROWS, w=MAP)
+                dst = grouped[:, g, :, :].rearrange("p (r w) t -> p r w t", r=ROWS, w=MAP)
+                nc.vector.tensor_copy(out=dst[:, :, 0 : MAP - SEAM, :], in_=src[:, :, SEAM:MAP, :])
+                nc.vector.tensor_copy(out=dst[:, :, MAP - SEAM : MAP, :], in_=src[:, :, 0:SEAM, :])
+            for g in range(PASSES):
+                for m in range(STRIP_TILES):
+                    nc.vector.quantize_mx(
+                        out=codes[:, g, P * m : P * (m + 1)].bitcast(FP8X4),
+                        scales=scales[:, g, P * m : P * (m + 1)],
+                        in_=grouped[:, g, P * m : P * (m + 1), :].rearrange("p a t -> p (a t)"),
+                    )
+            return codes, scales
+
+        def project(codes, scales, b, y0, y_last):
+            for m in range(STRIP_TILES):
+                acc = psum.tile([P, HID], F32, tag="bank")
+                for g in range(PASSES):
+                    nc.tensor.matmul_mx(
+                        out=acc[:],
+                        lhsT=codes[:, g, P * m : P * (m + 1)].bitcast(FP8X4),
+                        lhsT_scale=scales[:, g, P * m : P * (m + 1)],
+                        rhs=w1_codes[:, g, :].bitcast(FP8X4),
+                        rhs_scale=w1_scales[:, g, :],
+                        start=(g == 0),
+                        stop=(g == PASSES - 1),
+                    )
+                act = act_pool.tile([P, HID], F32, tag="act")
+                nc.vector.tensor_tensor(out=act[:], in0=acc[:], in1=bias_bc[:], op=ALU.add)
+                nc.scalar.activation(out=act[:], in_=act[:], func=ACT.Gelu)
+                row = y0 * MAP + P * m
+                head = P if y_last == y0 + ROWS - 1 else min(P * (m + 1), STRIP - MAP) - P * m
+                nc.scalar.dma_start(out=out[b, row : row + head, :], in_=act[0:head, :])
+                if head < P:
+                    nc.scalar.dma_start(out=out[b, y_last * MAP : (y_last + 1) * MAP, :], in_=act[head:P, :])
+
+        stages = []
+        for wrow in (1, 2, 3):
+            for half in range(2):
+                y0 = WS * wrow + ROWS * half - CROP
+                if y0 + ROWS <= MAP:
+                    stages.append(((wrow,), half, y0, y0 + ROWS - 1))
+        stages.append(((0, WINDOWS - 1), 2, 0, MAP - 1))
+
+        last_second_half = max(i for i, stage in enumerate(stages) if stage[1] == 1)
+        n_stages = len(stages)
+
+        def live(i):
+            return 0 <= i < n_stages
+
+        def sources_of(i):
+            wrows, half = stages[i][0], stages[i][1]
+            if half < 2:
+                return [(held[wrows[0]], whole[half], split[half], 0)]
+            return [(held[wrows[0]], whole[1], split[1], 1), (held[wrows[1]], None, orphan, 1 - ROWS)]
+
+        held = {1: windows}
+        x_of, x1_of, spare_of, stats_of, planes_of, codes_of = {0: x_next}, {}, {}, {}, {}, {}
+        runs = (range(0, 8), range(8, 12), range(12, 14), range(14, 16))
+        with tc.manual_schedule():
+            for fresh in range(n_stages + 2):
+                ripe, late = fresh - 1, fresh - 2
+                if live(fresh):
+                    x1_of[fresh] = x1_pool.tile([P, UNITS, C], F32, tag="x1", name="x1")
+
+                def mix_run(k):
+                    if live(fresh):
+                        mix(sources_of(fresh), stages[fresh][1], x_of[fresh], x1_of[fresh], runs[k])
+
+                if live(ripe):
+                    spare_of[ripe] = spare_pool.tile([P, C], F32, tag="spare", name="spare")
+                    for b in range(IMAGES):
+                        stats_of[ripe, b] = statistics(x1_of[ripe], x_of[ripe], b)
+                if live(fresh + 1):
+                    x_of[fresh + 1] = load_x(stages[fresh + 1][2], stages[fresh + 1][3])
+                if live(fresh + 2):
+                    for wrow in stages[fresh + 2][0]:
+                        if wrow not in held:
+                            held[wrow] = load_windows(wrow)
+                if live(late):
+                    codes_of[late, 1] = pack(planes_of[late, 1])
+                mix_run(0)
+                if live(late):
+                    project(codes_of[late, 1][0], codes_of[late, 1][1], 1, stages[late][2], stages[late][3])
+                if live(ripe):
+                    scale(x1_of[ripe], spare_of[ripe], 0, *stats_of[ripe, 0])
+                mix_run(1)
+                if live(ripe):
+                    planes_of[ripe, 0] = flip(x1_of[ripe], spare_of[ripe], 0)
+                    scale(x1_of[ripe], spare_of[ripe], 1, *stats_of[ripe, 1])
+                mix_run(2)
+                if live(ripe):
+                    planes_of[ripe, 1] = flip(x1_of[ripe], spare_of[ripe], 1)
+                    codes_of[ripe, 0] = pack(planes_of[ripe, 0])
+                mix_run(3)
+                if live(ripe):
+                    project(codes_of[ripe, 0][0], codes_of[ripe, 0][1], 0, stages[ripe][2], stages[ripe][3])
+                if fresh == 0:
+                    prepare_weights(1)
+                    prepare_w1()
+                if fresh == last_second_half:
+                    prepare_seam_weights()

@@ -35,6 +35,8 @@ STRIP = ROWS * MAP
 STRIP_TILES = STRIP // P
 MARGIN = 16
 SPLIT = LEFT + P
+QUAD = 4
+N_BLOCKS = 2 * HEADS
 
 FLOPS = 2 * HEADS * (WS * WS) * (WS * WS) * (IMAGES * WINDOWS * WINDOWS * HD) + 2 * IMAGES * MAP * MAP * C * HID
 
@@ -46,81 +48,340 @@ def tile_swinmlpblock_pa_t_kernel(tc, h_pad, x, sw, sb, g2, b2, w1, bb1, out):
         win_pool = ctx.enter_context(tc.tile_pool(name="windows", bufs=2))
         x_pool = ctx.enter_context(tc.tile_pool(name="x", bufs=2))
         x1_pool = ctx.enter_context(tc.tile_pool(name="x1", bufs=2))
-        small = ctx.enter_context(tc.tile_pool(name="small", bufs=3))
         spare_pool = ctx.enter_context(tc.tile_pool(name="spare", bufs=1))
+        small = ctx.enter_context(tc.tile_pool(name="small", bufs=3))
         plane_pool = ctx.enter_context(tc.tile_pool(name="planes", bufs=2))
         group_pool = ctx.enter_context(tc.tile_pool(name="grouped", bufs=2))
         code_pool = ctx.enter_context(tc.tile_pool(name="codes", bufs=2))
         act_pool = ctx.enter_context(tc.tile_pool(name="act", bufs=3))
-        psum = ctx.enter_context(tc.psum_pool(name="psum", bufs=8))
+        psum = ctx.enter_context(tc.psum_pool(name="psum", bufs=3))
+        psum_mx = ctx.enter_context(tc.psum_pool(name="psum_mx", bufs=2))
 
         win_view = h_pad.rearrange("b (wr r) (wc k q) c -> b wr wc r k (q c)", r=WS, wc=WINDOWS, k=WS // 2, q=2)
         x_view = x.rearrange("b (y w) c -> b w y c", w=MAP)
-
-        ident_f = const.tile([P, P], F32)
-        make_identity(nc, ident_f[:])
-        ident_b = const.tile([P, P], BF16)
-        make_identity(nc, ident_b[:])
-        by_rows = const.tile([P, ROWS, WS], F32)
-        nc.vector.tensor_copy(out=by_rows[:], in_=ident_f[:].rearrange("p (c r) -> p r c", c=WS, r=ROWS))
-        minus_half = const.tile([P, 2], F32)
-        nc.vector.memset(minus_half[:], -0.5)
+        sw_view = sw.rearrange("h (t p) j -> t p h j", t=2)
+        w1_view = w1.rearrange("(g p t) n -> g p t n", g=PASSES, t=PACK)
 
         def load_windows(wrow):
             inner = win_pool.tile([P, 4, 2, C], BF16, tag="inner")
             last = win_pool.tile([P, 2, 2, C], BF16, tag="last")
             first = win_pool.tile([P, 2, 2, C], BF16, tag="first")
+            loads = []
             for b in range(IMAGES):
                 for wcol in (1, 2):
-                    nc.sync.dma_start(
-                        out=inner[:, 2 * b + wcol - 1, :, :].rearrange("p q c -> p (q c)"),
-                        in_=win_view[b, wrow, wcol],
-                    )
+                    loads.append((inner[:, 2 * b + wcol - 1, :, :].rearrange("p q c -> p (q c)"), win_view[b, wrow, wcol]))
             for b in range(IMAGES):
-                nc.sync.dma_start(
-                    out=last[:, b, :, :].rearrange("p q c -> p (q c)"), in_=win_view[b, wrow, WINDOWS - 1]
-                )
-                nc.sync.dma_start(out=first[:, b, :, :].rearrange("p q c -> p (q c)"), in_=win_view[b, wrow, 0])
-            return inner, last, first
+                loads.append((last[:, b, :, :].rearrange("p q c -> p (q c)"), win_view[b, wrow, WINDOWS - 1]))
+                loads.append((first[:, b, :, :].rearrange("p q c -> p (q c)"), win_view[b, wrow, 0]))
+            return (inner, last, first), loads
 
         def load_x(y0, y_last):
             x_sb = x_pool.tile([P, UNITS, C], BF16, tag="x")
+            loads = []
             for b in range(IMAGES):
                 pieces = [(0, P, 2 * b + wcol - 1, WS * wcol - CROP) for wcol in (1, 2)]
                 pieces.append((0, LEFT, 4 + b, MAP - SEAM))
                 pieces.append((LEFT, P, 4 + b, 0))
                 for p0, p1, n, w0 in pieces:
                     w1_ = w0 + (p1 - p0) // ROWS
-                    nc.sync.dma_start(out=x_sb[p0:p1, n, :], in_=x_view[b, w0:w1_, y0 : y0 + ROWS, :])
+                    loads.append((x_sb[p0:p1, n, :], x_view[b, w0:w1_, y0 : y0 + ROWS, :]))
                     if y_last != y0 + ROWS - 1:
-                        nc.sync.dma_start(out=x_sb[p0 + ROWS - 1 : p1 : ROWS, n, :], in_=x_view[b, w0:w1_, y_last, :])
-            return x_sb
+                        loads.append((x_sb[p0 + ROWS - 1 : p1 : ROWS, n, :], x_view[b, w0:w1_, y_last, :]))
+            return x_sb, loads
 
-        sw_nat = x1_pool.tile([P, 2, HEADS, WS * WS], BF16, tag="x1")
-        sw_view = sw.rearrange("h (t p) j -> t p h j", t=2)
-        nc.sync.dma_start(out=sw_nat[:, 0], in_=sw_view[0])
-        windows = load_windows(1)
-        x_next = load_x(WS - CROP, WS - CROP + ROWS - 1)
-        nc.sync.dma_start(out=sw_nat[:, 1], in_=sw_view[1])
+        def load(to, source):
+            nc.sync.dma_start(out=to, in_=source)
 
         vec_rows = act_pool.tile([P, K_PASS], BF16, tag="act")
         nc.vector.memset(vec_rows[:].bitcast(I32), 0)
-        nc.scalar.dma_start(out=vec_rows[0:PASSES, :], in_=g2.rearrange("(g c) -> g c", c=K_PASS))
-        nc.scalar.dma_start(out=vec_rows[PASSES : 2 * PASSES, :], in_=b2.rearrange("(g c) -> g c", c=K_PASS))
-        vec_perm = act_pool.tile([P, PACK, P], BF16, tag="act")
-        nc.vector.tensor_copy(out=vec_perm[:], in_=vec_rows[:].rearrange("p (q t) -> p t q", t=PACK))
+        nc.sync.dma_start(out=vec_rows[0:PASSES, :], in_=g2.rearrange("(g c) -> g c", c=K_PASS))
+        nc.sync.dma_start(out=vec_rows[PASSES : 2 * PASSES, :], in_=b2.rearrange("(g c) -> g c", c=K_PASS))
         sb_rows = act_pool.tile([P, 2 * P], BF16, tag="act")
         nc.vector.memset(sb_rows[:].bitcast(I32), 0)
-        nc.scalar.dma_start(out=sb_rows[0:HEADS, :], in_=sb)
-        bias_bc = const.tile([P, HID], BF16)
-        nc.scalar.dma_start(out=bias_bc[:], in_=bb1.partition_broadcast(P))
-        sb_perm = act_pool.tile([P, 3, WS, ROWS], BF16, tag="act")
+        nc.sync.dma_start(out=sb_rows[0:HEADS, :], in_=sb)
+        bias_rows = group_pool.tile([P, HID], BF16, tag="grouped", align_bytes=64)
+        nc.vector.memset(bias_rows[:].bitcast(I32), 0)
+        nc.sync.dma_start(out=bias_rows[0:1, :], in_=bb1.rearrange("(o n) -> o n", o=1))
+
+        sw_nat = x1_pool.tile([P, 2, HEADS, WS * WS], BF16, tag="x1")
+        for quad in range(HEADS // QUAD):
+            hs = slice(QUAD * quad, QUAD * (quad + 1))
+            nc.sync.dma_start(out=sw_nat[:, 0, hs], in_=sw_view[0][:, hs])
+        windows, window_loads = load_windows(1)
+        x_next, x_loads = load_x(WS - CROP, WS - CROP + ROWS - 1)
+        for to, source in window_loads + x_loads:
+            load(to, source)
+        for quad in range(HEADS // QUAD):
+            hs = slice(QUAD * quad, QUAD * (quad + 1))
+            nc.sync.dma_start(out=sw_nat[:, 1, hs], in_=sw_view[1][:, hs])
+
+        ident_f = const.tile([P, P], F32)
+        make_identity(nc, ident_f[:])
+        ident_b = const.tile([P, P], BF16)
+        nc.vector.tensor_copy(out=ident_b[:], in_=ident_f[:])
+        warm = small.tile([P, 2], F32, tag="warm")
+        nc.scalar.activation(out=warm[:], in_=ident_f[:, 0:2], func=ACT.Gelu)
+        by_columns = ident_f[:].rearrange("p (c r) -> p r c", c=WS, r=ROWS)
+        by_rows = const.tile([P, ROWS, WS], F32)
+        nc.vector.tensor_copy(out=by_rows[:], in_=by_columns)
+        by_rows_seam = const.tile([P, ROWS, WS], F32)
+        nc.vector.tensor_copy(out=by_rows_seam[:, :, SEAM:], in_=by_columns[:, :, SEAM:])
+        nc.vector.tensor_copy(out=by_rows_seam[:, 1:, 0:SEAM], in_=by_columns[:, : ROWS - 1, 0:SEAM])
+        nc.vector.tensor_copy(out=by_rows_seam[:, 0:1, 0:SEAM], in_=by_columns[:, ROWS - 1 :, 0:SEAM])
+        to_tile = const.tile([P, WS, ROWS], BF16)
+        nc.vector.tensor_copy(out=to_tile[:], in_=ident_f[:].rearrange("p (r c) -> p c r", c=WS, r=ROWS))
+        minus_half = const.tile([P, 3], F32)
+        nc.vector.memset(minus_half[:], -0.5)
+        ones = act_pool.tile([P, P], BF16, tag="act")
+        nc.vector.memset(ones[:], 1.0)
+
+        whole = [const.tile([P, 2 * MARGIN + N_BLOCKS * P], BF16, name="whole%d" % half) for half in range(2)]
+        split = [const.tile([P, 2 * MARGIN + N_BLOCKS * SPLIT], BF16, name="split%d" % half) for half in range(2)]
+        orphan = const.tile([P, 2 * MARGIN + N_BLOCKS * P], BF16)
+        orphan_split = const.tile([P, 2 * MARGIN + N_BLOCKS * SPLIT], BF16)
+
+        def by_block(t, width):
+            return t[:, MARGIN : MARGIN + N_BLOCKS * width].rearrange("p (n m) -> p n m", m=width)
+
+        for t, width in ((whole[0], P), (split[0], SPLIT), (whole[1], P), (split[1], SPLIT)):
+            nc.vector.memset(t[:, 0:MARGIN].bitcast(I32), 0)
+            nc.vector.memset(t[:, MARGIN + N_BLOCKS * width :].bitcast(I32), 0)
+            if width == SPLIT:
+                nc.vector.memset(by_block(t, SPLIT)[:, :, LEFT : 2 * LEFT], 0.0)
+        nc.gpsimd.memset(orphan[:].bitcast(I32), 0)
+        nc.gpsimd.memset(orphan_split[:].bitcast(I32), 0)
+
+        def prepare_quad(half, quad, copy):
+            sw_ps = psum.tile([P, 2 * QUAD, P], BF16, tag="mix" if quad % 2 == 0 else "turn")
+            for i in range(2 * QUAD):
+                h, q = QUAD * quad + i // 2, i % 2
+                nc.tensor.transpose(
+                    out=sw_ps[:, i, :],
+                    in_=sw_nat[:, half, h, :].rearrange("p (k q) -> p q k", q=2)[:, q, :],
+                    identity=to_tile[:].rearrange("p c r -> p (c r)"),
+                )
+            ns = slice(2 * QUAD * quad, 2 * QUAD * (quad + 1))
+            src = by_block(whole[half], P)[:, ns, :]
+            dst = by_block(split[half], SPLIT)[:, ns, :]
+            copy(out=src, in_=sw_ps[:])
+            nc.vector.tensor_copy(out=dst[:, :, 0:LEFT], in_=src[:, :, 0:LEFT])
+            nc.vector.tensor_copy(out=dst[:, :, 2 * LEFT :], in_=src[:, :, LEFT:])
+
+        def first_rows(t, width, m0, m1):
+            return by_block(t, width)[:, :, m0:m1].rearrange("p n (c r) -> p n c r", r=ROWS)[:, :, :, 0:1]
+
+        def copy_row_8():
+            nc.gpsimd.tensor_copy(out=first_rows(orphan, P, 0, P), in_=first_rows(whole[1], P, 0, P))
+            nc.gpsimd.tensor_copy(out=first_rows(orphan_split, SPLIT, 0, LEFT), in_=first_rows(whole[1], P, 0, LEFT))
+            nc.gpsimd.tensor_copy(
+                out=first_rows(orphan_split, SPLIT, 2 * LEFT, SPLIT), in_=first_rows(whole[1], P, LEFT, P)
+            )
+
+        def clear_row_8():
+            nc.gpsimd.memset(first_rows(whole[1], P, 0, P), 0.0)
+            nc.gpsimd.memset(first_rows(split[1], SPLIT, 0, LEFT), 0.0)
+            nc.gpsimd.memset(first_rows(split[1], SPLIT, 2 * LEFT, SPLIT), 0.0)
+
+        w1_codes = const.tile([P, PASSES, HID], U32, align_bytes=64)
+        w1_scales = const.tile([P, PASSES, HID], U8, align_bytes=64)
+        w1_raw = {}
+
+        def load_w1(g):
+            w1_raw[g] = spare_pool.tile([P, PACK, HID], BF16, tag="spare", name="w1_raw")
+            nc.sync.dma_start(out=w1_raw[g][:], in_=w1_view[g])
+
+        def prepare_w1(g, half):
+            ns = slice(HID // 2 * half, HID // 2 * (half + 1))
+            grouped = group_pool.tile([P, HID // 2, PACK], BF16, tag="grouped", align_bytes=64)
+            nc.vector.tensor_copy(out=grouped[:], in_=w1_raw[g][:, :, ns].rearrange("p t n -> p n t"))
+            nc.vector.quantize_mx(
+                out=w1_codes[:, g, ns].bitcast(FP8X4),
+                scales=w1_scales[:, g, ns],
+                in_=grouped[:].rearrange("p n t -> p (n t)"),
+            )
+
+        def accumulate(acc, terms):
+            for i, (weights, moving) in enumerate(terms):
+                nc.tensor.matmul(out=acc, lhsT=weights, rhs=moving, start=(i == 0), stop=(i == len(terms) - 1))
+
+        def mix(sources, sb_index, x_sb, x1, h):
+            cols = slice(HD * h, HD * (h + 1))
+            inner_terms, seam_terms = [], []
+            for (inner, last, first), whole_w, split_w, start in sources:
+                for q in range(2):
+                    n = 2 * h + q
+                    w0 = MARGIN + P * n + start
+                    s0 = MARGIN + SPLIT * n + start
+                    inner_terms.append((whole_w[:, w0 : w0 + P], inner[:, :, q, cols]))
+                    seam_terms.append((split_w[:, s0 : s0 + P], last[:, :, q, cols]))
+                    seam_terms.append((split_w[:, s0 + LEFT : s0 + LEFT + P], first[:, :, q, cols]))
+            acc = psum.tile([P, UNITS, HD], F32, tag="mix")
+            accumulate(acc[:, 0:4, :], inner_terms)
+            accumulate(acc[:, 4:6, :], seam_terms)
+            nc.vector.scalar_tensor_tensor(
+                out=x1[:, :, cols],
+                in0=acc[:],
+                scalar=sb_col[:, sb_index, h : h + 1],
+                in1=x_sb[:, :, cols],
+                op0=ALU.add,
+                op1=ALU.add,
+            )
+
+        def units_of(b):
+            return (4 + b, 2 * b, 2 * b + 1)
+
+        def slots_of(st, b):
+            x1 = st["x1"]
+            if b == 0:
+                return st["spare"][:], x1[:, 4, :], x1[:, 0, :]
+            return x1[:, 1, :], x1[:, 5, :], x1[:, 2, :]
+
+        def open_statistics(st, b, on_vector):
+            st["on_vector", b] = on_vector
+            st["mean_var", b] = small.tile([P, 3, 2], F32, tag="mean_var", name="mean_var")
+            st["neg_mean", b] = small.tile([P, 3], F32, tag="neg_mean", name="neg_mean")
+            st["squares", b] = small.tile([P, 3], F32, tag="squares", name="squares")
+            st["rstd", b] = small.tile([P, 3], F32, tag="rstd", name="rstd")
+
+        def moments(st, b, j):
+            x1 = st["x1"][:, units_of(b)[j], :]
+            stats = small.tile([P, 2, 6], F32, tag="stats")
+            for i in range(2):
+                nc.vector.bn_stats(out=stats[:, i, :], in_=x1[:, 512 * i : 512 * (i + 1)])
+            nc.vector.bn_aggr(out=st["mean_var", b][:, j, :], in_=stats[:])
+
+        def negative_mean(st, b, j):
+            nc.scalar.activation(
+                out=unread[:],
+                in_=st["x1"][:, units_of(b)[j], :],
+                func=ACT.Identity,
+                scale=-1.0 / C,
+                accum_out=st["neg_mean", b][:, j : j + 1],
+            )
+
+        def squared_distances(st, b, j):
+            nc.scalar.activation(
+                out=unread[:],
+                in_=st["x1"][:, units_of(b)[j], :],
+                func=ACT.Square,
+                bias=st["neg_mean", b][:, j : j + 1],
+                accum_out=st["squares", b][:, j : j + 1],
+            )
+
+        def inverse_deviation(st, b):
+            nv, rstd = st["on_vector", b], st["rstd", b]
+            if nv > 0:
+                nc.gpsimd.tensor_scalar(
+                    out=rstd[:, 0:nv],
+                    in0=st["mean_var", b][:, 0:nv, 1],
+                    scalar1=1.0,
+                    scalar2=EPS,
+                    op0=ALU.mult,
+                    op1=ALU.add,
+                )
+            nc.gpsimd.tensor_scalar(
+                out=rstd[:, nv:3],
+                in0=st["squares", b][:, nv:3],
+                scalar1=1.0 / C,
+                scalar2=EPS,
+                op0=ALU.mult,
+                op1=ALU.add,
+            )
+            nc.gpsimd.tensor_tensor(out=rstd[:], in0=rstd[:], in1=minus_half[:], op=ALU.pow)
+
+        def scale(st, b, j):
+            if j < st["on_vector", b]:
+                mean, op = st["mean_var", b][:, j, 0:1], ALU.subtract
+            else:
+                mean, op = st["neg_mean", b][:, j : j + 1], ALU.add
+            nc.vector.tensor_scalar(
+                out=slots_of(st, b)[j].rearrange("p (g t q) -> p g q t", g=PASSES, t=PACK),
+                in0=st["x1"][:, units_of(b)[j], :].rearrange("p (g q t) -> p g q t", g=PASSES, t=PACK),
+                scalar1=mean,
+                scalar2=st["rstd", b][:, j : j + 1],
+                op0=op,
+                op1=ALU.mult,
+            )
+
+        def turn(st, b, k, on_vector):
+            g, t = divmod(k, PACK)
+            if t == 0:
+                st["planes", b, g] = plane_pool.tile([P, PACK, STRIP], BF16, tag="planes", name="planes")
+            turned = psum.tile([P, ROWS, MAP], F32, tag="turn")
+            for i, y in enumerate(slots_of(st, b)):
+                nc.tensor.transpose(
+                    out=turned[:, :, WS * i : WS * (i + 1)],
+                    in_=y[:, P * k : P * (k + 1)],
+                    identity=by_rows_seam[:] if i == 0 else by_rows[:],
+                )
+            gain, shift = gain_shift[:, k : k + 1], gain_shift[:, BLOCKS + k : BLOCKS + k + 1]
+            src, dst = turned[:].rearrange("p r w -> p (r w)"), st["planes", b, g][:, t, :]
+            if on_vector:
+                nc.vector.tensor_scalar(out=dst, in0=src, scalar1=gain, scalar2=shift, op0=ALU.mult, op1=ALU.add)
+            else:
+                nc.scalar.activation(out=dst, in_=src, func=ACT.Identity, scale=gain, bias=shift)
+
+        def pack(st, b, g):
+            st["grouped", b, g] = group_pool.tile([P, STRIP, PACK], BF16, tag="grouped", name="grouped", align_bytes=64)
+            nc.vector.tensor_copy(
+                out=st["grouped", b, g][:].rearrange("p (c i) t -> p c t i", i=4),
+                in_=st["planes", b, g][:].rearrange("p t (c i) -> p c t i", i=4),
+            )
+
+        def quantise(st, b, g):
+            if g == 0:
+                st["codes", b] = code_pool.tile([P, PASSES, STRIP], U32, tag="codes", name="codes", align_bytes=64)
+                st["scales", b] = code_pool.tile([P, PASSES, STRIP], U8, tag="scales", name="scales", align_bytes=64)
+            for m0, m1 in ((0, 2 * P), (2 * P, 3 * P)):
+                nc.vector.quantize_mx(
+                    out=st["codes", b][:, g, m0:m1].bitcast(FP8X4),
+                    scales=st["scales", b][:, g, m0:m1],
+                    in_=st["grouped", b, g][:, m0:m1, :].rearrange("p a t -> p (a t)"),
+                )
+
+        def project(st, b, m):
+            acc = psum_mx.tile([P, HID], F32, tag="mx", name="acc")
+            for g in range(PASSES):
+                nc.tensor.matmul_mx(
+                    out=acc[:],
+                    lhsT=st["codes", b][:, g, P * m : P * (m + 1)].bitcast(FP8X4),
+                    lhsT_scale=st["scales", b][:, g, P * m : P * (m + 1)],
+                    rhs=w1_codes[:, g, :].bitcast(FP8X4),
+                    rhs_scale=w1_scales[:, g, :],
+                    start=(g == 0),
+                    stop=(g == PASSES - 1),
+                )
+            st["acc", b, m] = acc
+
+        def finish(st, b, m):
+            act = act_pool.tile([P, HID], F32, tag="act")
+            nc.vector.tensor_tensor(out=act[:], in0=st["acc", b, m][:], in1=bias_bc[:], op=ALU.add)
+            nc.scalar.activation(out=act[:], in_=act[:], func=ACT.Gelu)
+            y0, y_last = st["rows"]
+            pieces = []
+            if m == 0:
+                pieces.append((0, SEAM, y_last * MAP + MAP - SEAM))
+            p0, p1 = max(P * m, SEAM), P * (m + 1)
+            cut = min(max(SEAM + STRIP - MAP, p0), p1)
+            pieces.append((p0, cut, y0 * MAP + p0 - SEAM))
+            pieces.append((cut, p1, y_last * MAP + cut - SEAM - (STRIP - MAP)))
+            for s0, s1, row in pieces:
+                mid = s0 + (s1 - s0) // 16 * 16
+                for a, z in ((s0, mid), (mid, s1)):
+                    if a < z:
+                        nc.sync.dma_start(
+                            out=out[b, row + a - s0 : row + z - s0, :], in_=act[a - P * m : z - P * m, :]
+                        )
+
+        vec_perm = plane_pool.tile([P, PACK, P], BF16, tag="planes")
+        nc.vector.tensor_copy(out=vec_perm[:], in_=vec_rows[:].rearrange("p (q t) -> p t q", t=PACK))
+        sb_perm = plane_pool.tile([P, 3, WS, ROWS], BF16, tag="planes")
         nc.vector.tensor_copy(
             out=sb_perm[:, 0:2, :, :], in_=sb_rows[:].rearrange("p (t r c) -> p t c r", t=2, r=ROWS, c=WS)
         )
         nc.vector.tensor_copy(out=sb_perm[:, 2, :, 0 : ROWS - 1], in_=sb_perm[:, 1, :, 1:ROWS])
         nc.vector.tensor_copy(out=sb_perm[:, 2, :, ROWS - 1 : ROWS], in_=sb_perm[:, 1, :, 0:1])
-        vec_ps = psum.tile([P, PACK + 3, P], BF16, tag="bank")
+        vec_ps = psum_mx.tile([P, PACK + 3, P], BF16, tag="mx")
         for t in range(PACK):
             nc.tensor.transpose(out=vec_ps[:, t, :], in_=vec_perm[:, t, :], identity=ident_b[:])
         for i in range(3):
@@ -134,232 +395,13 @@ def tile_swinmlpblock_pa_t_kernel(tc, h_pad, x, sw, sb, g2, b2, w1, bb1, out):
         )
         sb_col = const.tile([P, 3, HEADS], F32)
         nc.vector.tensor_copy(out=sb_col[:], in_=vec_ps[:, PACK : PACK + 3, 0:HEADS])
-
-        n_blocks = 2 * HEADS
-        whole = [const.tile([P, 2 * MARGIN + n_blocks * P], BF16, name="whole%d" % half) for half in range(2)]
-        split = [const.tile([P, 2 * MARGIN + n_blocks * SPLIT], BF16, name="split%d" % half) for half in range(2)]
-        orphan = const.tile([P, 2 * MARGIN + n_blocks * SPLIT], BF16)
-        for t in whole:
-            nc.vector.memset(t[:, 0:MARGIN].bitcast(I32), 0)
-            nc.vector.memset(t[:, MARGIN + n_blocks * P :].bitcast(I32), 0)
-        for t in split + [orphan]:
-            nc.vector.memset(t[:].bitcast(I32), 0)
-
-        def by_block(t, width):
-            return t[:, MARGIN : MARGIN + n_blocks * width].rearrange("p (n m) -> p n m", m=width)
-
-        def prepare_weights(half):
-            for quad in range(HEADS // 4):
-                sw_ps = psum.tile([P, 8, P], BF16, tag="bank")
-                for i in range(8):
-                    h, q = 4 * quad + i // 2, i % 2
-                    nc.tensor.transpose(
-                        out=sw_ps[:, i, :],
-                        in_=sw_nat[:, half, h, :].rearrange("p (k q) -> p q k", q=2)[:, q, :],
-                        identity=ident_b[:],
-                    )
-                dst = by_block(whole[half], P)[:, 8 * quad : 8 * (quad + 1), :].rearrange(
-                    "p n (c r) -> p n c r", c=WS, r=ROWS
-                )
-                src = sw_ps[:].rearrange("p n (r c) -> p n c r", r=ROWS, c=WS)
-                if quad % 2 == 0:
-                    nc.vector.tensor_copy(out=dst, in_=src)
-                else:
-                    nc.scalar.copy(out=dst, in_=src)
-            nc.vector.tensor_copy(out=by_block(split[half], SPLIT)[:, :, 0:LEFT], in_=by_block(whole[half], P)[:, :, 0:LEFT])
-            nc.vector.tensor_copy(
-                out=by_block(split[half], SPLIT)[:, :, 2 * LEFT : SPLIT], in_=by_block(whole[half], P)[:, :, LEFT:P]
-            )
-
-        def first_rows(t, width, m0, m1):
-            return by_block(t, width)[:, :, m0:m1].rearrange("p n (c r) -> p n c r", r=ROWS)[:, :, :, 0:1]
-
-        def prepare_seam_weights():
-            nc.gpsimd.tensor_copy(out=first_rows(orphan, SPLIT, 0, LEFT), in_=first_rows(split[1], SPLIT, 0, LEFT))
-            nc.gpsimd.tensor_copy(
-                out=first_rows(orphan, SPLIT, 2 * LEFT, SPLIT), in_=first_rows(split[1], SPLIT, 2 * LEFT, SPLIT)
-            )
-            nc.gpsimd.memset(first_rows(whole[1], P, 0, P), 0.0)
-            nc.gpsimd.memset(first_rows(split[1], SPLIT, 0, LEFT), 0.0)
-            nc.gpsimd.memset(first_rows(split[1], SPLIT, 2 * LEFT, SPLIT), 0.0)
-
-        prepare_weights(0)
-
-        w1_codes = const.tile([P, PASSES, HID], U32, align_bytes=64)
-        w1_scales = const.tile([P, PASSES, HID], U8, align_bytes=64)
-
-        def prepare_w1():
-            w1_view = w1.rearrange("(g p t) n -> g p t n", g=PASSES, t=PACK)
-            for g in range(PASSES):
-                raw = plane_pool.tile([P, PACK, HID], BF16, tag="planes")
-                nc.sync.dma_start(out=raw[:], in_=w1_view[g])
-                grouped = group_pool.tile([P, HID, PACK], BF16, tag="grouped", align_bytes=64)
-                nc.vector.tensor_copy(out=grouped[:], in_=raw[:].rearrange("p t n -> p n t"))
-                nc.vector.quantize_mx(
-                    out=w1_codes[:, g, :].bitcast(FP8X4),
-                    scales=w1_scales[:, g, :],
-                    in_=grouped[:].rearrange("p n t -> p (n t)"),
-                )
-
-        def accumulate(acc, terms):
-            for i, (weights, moving) in enumerate(terms):
-                nc.tensor.matmul(out=acc, lhsT=weights, rhs=moving, start=(i == 0), stop=(i == len(terms) - 1))
-
-        def mix(sources, sb_index, x_sb, x1, heads):
-            for h in heads:
-                cols = slice(HD * h, HD * (h + 1))
-                inner_terms, seam_terms = [], []
-                for (inner, last, first), whole_w, split_w, start in sources:
-                    for q in range(2):
-                        n = 2 * h + q
-                        s0 = MARGIN + SPLIT * n + start
-                        left_w = split_w[:, s0 : s0 + P]
-                        right_w = split_w[:, s0 + LEFT : s0 + LEFT + P]
-                        if whole_w is None:
-                            inner_terms.append((left_w, inner[:, :, q, cols]))
-                            inner_terms.append((right_w, inner[:, :, q, cols]))
-                        else:
-                            w0 = MARGIN + P * n + start
-                            inner_terms.append((whole_w[:, w0 : w0 + P], inner[:, :, q, cols]))
-                        seam_terms.append((left_w, last[:, :, q, cols]))
-                        seam_terms.append((right_w, first[:, :, q, cols]))
-                acc = psum.tile([P, UNITS, HD], F32, tag="bank")
-                accumulate(acc[:, 0:4, :], inner_terms)
-                accumulate(acc[:, 4:6, :], seam_terms)
-                nc.vector.scalar_tensor_tensor(
-                    out=x1[:, :, cols],
-                    in0=acc[:],
-                    scalar=sb_col[:, sb_index, h : h + 1],
-                    in1=x_sb[:, :, cols],
-                    op0=ALU.add,
-                    op1=ALU.add,
-                )
-
-        def statistics(x1, x_sb, b):
-            seam, inner = 4 + b, (2 * b, 2 * b + 1)
-            stats = small.tile([P, 2, 6], F32, tag="stats")
-            for i in range(2):
-                nc.vector.bn_stats(out=stats[:, i, :], in_=x1[:, seam, 512 * i : 512 * (i + 1)])
-            mean_var = small.tile([P, 2], F32, tag="mean_var")
-            nc.vector.bn_aggr(out=mean_var[:], in_=stats[:])
-            sums = small.tile([P, 2], F32, tag="sums")
-            for j, n in enumerate(inner):
-                nc.scalar.activation(out=x_sb[:, n, :], in_=x1[:, n, :], func=ACT.Identity, accum_out=sums[:, j : j + 1])
-            neg_mean = small.tile([P, 2], F32, tag="neg_mean")
-            nc.scalar.mul(out=neg_mean[:], in_=sums[:], mul=-1.0 / C)
-            squares = small.tile([P, 2], F32, tag="squares")
-            for j, n in enumerate(inner):
-                nc.scalar.activation(
-                    out=x_sb[:, n, :],
-                    in_=x1[:, n, :],
-                    func=ACT.Square,
-                    bias=neg_mean[:, j : j + 1],
-                    accum_out=squares[:, j : j + 1],
-                )
-            return mean_var, neg_mean, squares
-
-        def slots(x1, spare, b):
-            if b == 0:
-                return spare[:], x1[:, 4, :], x1[:, 0, :]
-            return x1[:, 1, :], x1[:, 5, :], x1[:, 2, :]
-
-        def permuted(slot):
-            return slot.rearrange("p (g t q) -> p g q t", g=PASSES, t=PACK)
-
-        def scale(x1, spare, b, mean_var, neg_mean, squares):
-            seam, inner = 4 + b, (2 * b, 2 * b + 1)
-            to = slots(x1, spare, b)
-            seam_scalars = small.tile([P, 2], F32, tag="seam_scalars")
-            nc.gpsimd.tensor_scalar(
-                out=seam_scalars[:, 0:1], in0=mean_var[:, 0:1], scalar1=-1.0, scalar2=0.0, op0=ALU.mult, op1=ALU.add
-            )
-            nc.gpsimd.tensor_scalar(
-                out=seam_scalars[:, 1:2], in0=mean_var[:, 1:2], scalar1=1.0, scalar2=EPS, op0=ALU.mult, op1=ALU.add
-            )
-            nc.gpsimd.tensor_tensor(
-                out=seam_scalars[:, 1:2], in0=seam_scalars[:, 1:2], in1=minus_half[:, 0:1], op=ALU.pow
-            )
-            rstd = small.tile([P, 2], F32, tag="rstd")
-            nc.gpsimd.tensor_scalar(
-                out=rstd[:], in0=squares[:], scalar1=1.0 / C, scalar2=EPS, op0=ALU.mult, op1=ALU.add
-            )
-            nc.gpsimd.tensor_tensor(out=rstd[:], in0=rstd[:], in1=minus_half[:], op=ALU.pow)
-            nc.vector.tensor_scalar(
-                out=permuted(to[0]),
-                in0=x1[:, seam, :].rearrange("p (g q t) -> p g q t", g=PASSES, t=PACK),
-                scalar1=seam_scalars[:, 0:1],
-                scalar2=seam_scalars[:, 1:2],
-                op0=ALU.add,
-                op1=ALU.mult,
-            )
-            for j, n in enumerate(inner):
-                nc.vector.tensor_scalar(
-                    out=permuted(to[1 + j]),
-                    in0=x1[:, n, :].rearrange("p (g q t) -> p g q t", g=PASSES, t=PACK),
-                    scalar1=neg_mean[:, j : j + 1],
-                    scalar2=rstd[:, j : j + 1],
-                    op0=ALU.add,
-                    op1=ALU.mult,
-                )
-
-        def flip(x1, spare, b):
-            planes = plane_pool.tile([P, BLOCKS, 3 * P], BF16, tag="planes")
-            for k in range(BLOCKS):
-                turned = psum.tile([P, ROWS, MAP], F32, tag="bank")
-                for slot, y in enumerate(slots(x1, spare, b)):
-                    nc.tensor.transpose(
-                        out=turned[:, :, WS * slot : WS * (slot + 1)],
-                        in_=y[:, P * k : P * (k + 1)],
-                        identity=by_rows[:],
-                    )
-                nc.scalar.activation(
-                    out=planes[:, k, :],
-                    in_=turned[:].rearrange("p r w -> p (r w)"),
-                    func=ACT.Identity,
-                    scale=gain_shift[:, k : k + 1],
-                    bias=gain_shift[:, BLOCKS + k : BLOCKS + k + 1],
-                )
-            return planes
-
-        def pack(planes):
-            grouped = group_pool.tile([P, PASSES, STRIP, PACK], BF16, tag="grouped", align_bytes=64)
-            codes = code_pool.tile([P, PASSES, STRIP], U32, tag="codes", align_bytes=64)
-            scales = code_pool.tile([P, PASSES, STRIP], U8, tag="scales", align_bytes=64)
-            for g in range(PASSES):
-                src = planes[:, PACK * g : PACK * (g + 1), :].rearrange("p t (r w) -> p r w t", r=ROWS, w=MAP)
-                dst = grouped[:, g, :, :].rearrange("p (r w) t -> p r w t", r=ROWS, w=MAP)
-                nc.vector.tensor_copy(out=dst[:, :, 0 : MAP - SEAM, :], in_=src[:, :, SEAM:MAP, :])
-                nc.vector.tensor_copy(out=dst[:, :, MAP - SEAM : MAP, :], in_=src[:, :, 0:SEAM, :])
-            for g in range(PASSES):
-                for m in range(STRIP_TILES):
-                    nc.vector.quantize_mx(
-                        out=codes[:, g, P * m : P * (m + 1)].bitcast(FP8X4),
-                        scales=scales[:, g, P * m : P * (m + 1)],
-                        in_=grouped[:, g, P * m : P * (m + 1), :].rearrange("p a t -> p (a t)"),
-                    )
-            return codes, scales
-
-        def project(codes, scales, b, y0, y_last):
-            for m in range(STRIP_TILES):
-                acc = psum.tile([P, HID], F32, tag="bank")
-                for g in range(PASSES):
-                    nc.tensor.matmul_mx(
-                        out=acc[:],
-                        lhsT=codes[:, g, P * m : P * (m + 1)].bitcast(FP8X4),
-                        lhsT_scale=scales[:, g, P * m : P * (m + 1)],
-                        rhs=w1_codes[:, g, :].bitcast(FP8X4),
-                        rhs_scale=w1_scales[:, g, :],
-                        start=(g == 0),
-                        stop=(g == PASSES - 1),
-                    )
-                act = act_pool.tile([P, HID], F32, tag="act")
-                nc.vector.tensor_tensor(out=act[:], in0=acc[:], in1=bias_bc[:], op=ALU.add)
-                nc.scalar.activation(out=act[:], in_=act[:], func=ACT.Gelu)
-                row = y0 * MAP + P * m
-                head = P if y_last == y0 + ROWS - 1 else min(P * (m + 1), STRIP - MAP) - P * m
-                nc.scalar.dma_start(out=out[b, row : row + head, :], in_=act[0:head, :])
-                if head < P:
-                    nc.scalar.dma_start(out=out[b, y_last * MAP : (y_last + 1) * MAP, :], in_=act[head:P, :])
+        bias_ps = psum_mx.tile([P, HID], F32, tag="mx")
+        nc.tensor.matmul(out=bias_ps[:], lhsT=ones[:], rhs=bias_rows[:], start=True, stop=True)
+        bias_bc = const.tile([P, HID], BF16)
+        nc.vector.tensor_copy(out=bias_bc[:], in_=bias_ps[:])
+        for quad in range(HEADS // QUAD):
+            prepare_quad(0, quad, nc.vector.tensor_copy if quad % 2 == 0 else nc.scalar.copy)
+        unread = const.tile([P, C], BF16)
 
         stages = []
         for wrow in (1, 2, 3):
@@ -368,62 +410,108 @@ def tile_swinmlpblock_pa_t_kernel(tc, h_pad, x, sw, sb, g2, b2, w1, bb1, out):
                 if y0 + ROWS <= MAP:
                     stages.append(((wrow,), half, y0, y0 + ROWS - 1))
         stages.append(((0, WINDOWS - 1), 2, 0, MAP - 1))
-
-        last_second_half = max(i for i, stage in enumerate(stages) if stage[1] == 1)
         n_stages = len(stages)
+        last_second_half = max(i for i, stage in enumerate(stages) if stage[1] == 1)
 
         def live(i):
             return 0 <= i < n_stages
+
+        held = {1: windows}
 
         def sources_of(i):
             wrows, half = stages[i][0], stages[i][1]
             if half < 2:
                 return [(held[wrows[0]], whole[half], split[half], 0)]
-            return [(held[wrows[0]], whole[1], split[1], 1), (held[wrows[1]], None, orphan, 1 - ROWS)]
+            return [(held[wrows[0]], whole[1], split[1], 1), (held[wrows[1]], orphan, orphan_split, 1 - ROWS)]
 
-        held = {1: windows}
-        x_of, x1_of, spare_of, stats_of, planes_of, codes_of = {0: x_next}, {}, {}, {}, {}, {}
-        runs = (range(0, 8), range(8, 12), range(12, 14), range(14, 16))
-        with tc.manual_schedule():
+        fetch_round = {2: 0, 3: 2, 0: 4}
+
+        def older_work(ripe, late):
+            at = [[] for i in range(HEADS)]
+            if late is not None:
+                at[0].append((finish, late, 0, 1))
+                at[0].append((pack, late, 1, 0))
+                at[1].append((finish, late, 0, 2))
+            if ripe is not None:
+                alone = ripe is states.get(n_stages - 1)
+                open_statistics(ripe, 0, 1)
+                open_statistics(ripe, 1, 2 if alone else 0)
+                for b in range(IMAGES):
+                    for j in range(ripe["on_vector", b]):
+                        at[b + j].append((moments, ripe, b, j))
+                for j in (1, 2):
+                    at[0].append((negative_mean, ripe, 0, j))
+                for j in (1, 2):
+                    at[1].append((squared_distances, ripe, 0, j))
+                at[2].append((inverse_deviation, ripe, 0))
+                scalar_tiles = range(ripe["on_vector", 1], 3)
+                for i, j in enumerate(scalar_tiles):
+                    at[3 + i].append((negative_mean, ripe, 1, j))
+                for i, j in enumerate(scalar_tiles):
+                    at[7 + i].append((squared_distances, ripe, 1, j))
+                at[4].append((scale, ripe, 0, 0))
+                at[5].append((scale, ripe, 0, 1))
+                at[5].append((scale, ripe, 0, 2))
+                for k in range(BLOCKS):
+                    at[6 + k // 2].append((turn, ripe, 0, k, alone and k % 2 == 1))
+                at[9].append((pack, ripe, 0, 0))
+                at[10].append((inverse_deviation, ripe, 1))
+                at[10].append((pack, ripe, 0, 1))
+                at[11].append((scale, ripe, 1, 0))
+                at[11].append((scale, ripe, 1, 1))
+                at[12].append((scale, ripe, 1, 2))
+                at[12].append((quantise, ripe, 0, 0))
+                at[13].append((quantise, ripe, 0, 1))
+                for k in range(BLOCKS):
+                    at[13 + k // 3].append((turn, ripe, 1, k, alone and k % 2 == 1))
+                for m in range(STRIP_TILES):
+                    at[(14, 15, 15)[m]].append((project, ripe, 0, m))
+                at[15].append((finish, ripe, 0, 0))
+            if late is not None:
+                at[1].append((pack, late, 1, 1))
+                at[2].append((quantise, late, 1, 0))
+                at[3].append((quantise, late, 1, 1))
+                for m in range(STRIP_TILES):
+                    at[4 + m].append((project, late, 1, m))
+                    at[5 + m].append((finish, late, 1, m))
+            return at
+
+        states = {}
+        x_of = {0: x_next}
+        with tc.manual_schedule(engines={mybir.EngineType.SP}):
             for fresh in range(n_stages + 2):
-                ripe, late = fresh - 1, fresh - 2
                 if live(fresh):
-                    x1_of[fresh] = x1_pool.tile([P, UNITS, C], F32, tag="x1", name="x1")
-
-                def mix_run(k):
-                    if live(fresh):
-                        mix(sources_of(fresh), stages[fresh][1], x_of[fresh], x1_of[fresh], runs[k])
-
-                if live(ripe):
-                    spare_of[ripe] = spare_pool.tile([P, C], F32, tag="spare", name="spare")
-                    for b in range(IMAGES):
-                        stats_of[ripe, b] = statistics(x1_of[ripe], x_of[ripe], b)
+                    states[fresh] = {
+                        "x1": x1_pool.tile([P, UNITS, C], F32, tag="x1", name="x1"),
+                        "rows": stages[fresh][2:],
+                    }
+                if live(fresh - 1):
+                    states[fresh - 1]["spare"] = spare_pool.tile([P, C], F32, tag="spare", name="spare")
+                at = older_work(states.get(fresh - 1) if live(fresh - 1) else None, states.get(fresh - 2) if live(fresh - 2) else None)
                 if live(fresh + 1):
-                    x_of[fresh + 1] = load_x(stages[fresh + 1][2], stages[fresh + 1][3])
-                if live(fresh + 2):
-                    for wrow in stages[fresh + 2][0]:
-                        if wrow not in held:
-                            held[wrow] = load_windows(wrow)
-                if live(late):
-                    codes_of[late, 1] = pack(planes_of[late, 1])
-                mix_run(0)
-                if live(late):
-                    project(codes_of[late, 1][0], codes_of[late, 1][1], 1, stages[late][2], stages[late][3])
-                if live(ripe):
-                    scale(x1_of[ripe], spare_of[ripe], 0, *stats_of[ripe, 0])
-                mix_run(1)
-                if live(ripe):
-                    planes_of[ripe, 0] = flip(x1_of[ripe], spare_of[ripe], 0)
-                    scale(x1_of[ripe], spare_of[ripe], 1, *stats_of[ripe, 1])
-                mix_run(2)
-                if live(ripe):
-                    planes_of[ripe, 1] = flip(x1_of[ripe], spare_of[ripe], 1)
-                    codes_of[ripe, 0] = pack(planes_of[ripe, 0])
-                mix_run(3)
-                if live(ripe):
-                    project(codes_of[ripe, 0][0], codes_of[ripe, 0][1], 0, stages[ripe][2], stages[ripe][3])
+                    x_of[fresh + 1], loads = load_x(stages[fresh + 1][2], stages[fresh + 1][3])
+                    for i, (to, source) in enumerate(loads):
+                        at[i * HEADS // len(loads)].append((load, to, source))
+                for wrow, fetched in fetch_round.items():
+                    if fetched == fresh:
+                        held[wrow], loads = load_windows(wrow)
+                        for i, (to, source) in enumerate(loads):
+                            at[2 * i].append((load, to, source))
                 if fresh == 0:
-                    prepare_weights(1)
-                    prepare_w1()
-                if fresh == last_second_half:
-                    prepare_seam_weights()
+                    load_w1(0)
+                    for quad in range(HEADS // QUAD):
+                        at[3 + 2 * quad].append((prepare_quad, 1, quad, nc.scalar.copy))
+                    at[10].append((prepare_w1, 0, 0))
+                    at[11].append((prepare_w1, 0, 1))
+                    at[11].append((load_w1, 1))
+                    at[14].append((prepare_w1, 1, 0))
+                    at[15].append((prepare_w1, 1, 1))
+                if fresh == 1:
+                    at[15].append((copy_row_8,))
+                if fresh == last_second_half + 1:
+                    at[11].append((clear_row_8,))
+                for h in range(HEADS):
+                    if live(fresh):
+                        mix(sources_of(fresh), stages[fresh][1], x_of[fresh], states[fresh]["x1"], h)
+                    for call in at[h]:
+                        call[0](*call[1:])

from contextlib import ExitStack

import concourse.mybir as mybir
from concourse.masks import make_identity

F32 = mybir.dt.float32
BF16 = mybir.dt.bfloat16
I32 = mybir.dt.int32
U32 = mybir.dt.uint32
U8 = mybir.dt.uint8
FP8X4 = mybir.dt.float8_e4m3fn_x4
ALU = mybir.AluOpType
ACT = mybir.ActivationFunctionType

P = 128
IMAGES = 2
WS = 16
WINDOWS = 4
CROP = 9
MAP = 48
C = 1024
HEADS = 16
HD = C // HEADS
HID = 512
EPS = 1e-5
ROWS = 8
SEAM = CROP + MAP - WS * (WINDOWS - 1)
LEFT = SEAM * ROWS
UNITS = 6
PACK = 4
K_PASS = P * PACK
PASSES = C // K_PASS
BLOCKS = C // P
STRIP = ROWS * MAP
STRIP_TILES = STRIP // P
MARGIN = 16
SPLIT = LEFT + P
QUAD = 4
N_BLOCKS = 2 * HEADS

FLOPS = 2 * HEADS * (WS * WS) * (WS * WS) * (IMAGES * WINDOWS * WINDOWS * HD) + 2 * IMAGES * MAP * MAP * C * HID


def tile_swinmlpblock_pa_t_kernel(tc, h_pad, x, sw, sb, g2, b2, w1, bb1, out):
    nc = tc.nc
    with ExitStack() as ctx:
        const = ctx.enter_context(tc.tile_pool(name="const", bufs=1))
        win_pool = ctx.enter_context(tc.tile_pool(name="windows", bufs=2))
        x_pool = ctx.enter_context(tc.tile_pool(name="x", bufs=2))
        x1_pool = ctx.enter_context(tc.tile_pool(name="x1", bufs=2))
        spare_pool = ctx.enter_context(tc.tile_pool(name="spare", bufs=1))
        small = ctx.enter_context(tc.tile_pool(name="small", bufs=3))
        plane_pool = ctx.enter_context(tc.tile_pool(name="planes", bufs=2))
        group_pool = ctx.enter_context(tc.tile_pool(name="grouped", bufs=2))
        code_pool = ctx.enter_context(tc.tile_pool(name="codes", bufs=2))
        act_pool = ctx.enter_context(tc.tile_pool(name="act", bufs=3))
        psum = ctx.enter_context(tc.psum_pool(name="psum", bufs=3))
        psum_mx = ctx.enter_context(tc.psum_pool(name="psum_mx", bufs=2))

        win_view = h_pad.rearrange("b (wr r) (wc k q) c -> b wr wc r k (q c)", r=WS, wc=WINDOWS, k=WS // 2, q=2)
        x_view = x.rearrange("b (y w) c -> b w y c", w=MAP)
        sw_view = sw.rearrange("h (t p) j -> t p h j", t=2)
        w1_view = w1.rearrange("(g p t) n -> g p t n", g=PASSES, t=PACK)

        def load_windows(wrow):
            inner = win_pool.tile([P, 4, 2, C], BF16, tag="inner")
            last = win_pool.tile([P, 2, 2, C], BF16, tag="last")
            first = win_pool.tile([P, 2, 2, C], BF16, tag="first")
            loads = []
            for b in range(IMAGES):
                for wcol in (1, 2):
                    loads.append((inner[:, 2 * b + wcol - 1, :, :].rearrange("p q c -> p (q c)"), win_view[b, wrow, wcol]))
            for b in range(IMAGES):
                loads.append((last[:, b, :, :].rearrange("p q c -> p (q c)"), win_view[b, wrow, WINDOWS - 1]))
                loads.append((first[:, b, :, :].rearrange("p q c -> p (q c)"), win_view[b, wrow, 0]))
            return (inner, last, first), loads

        def load_x(y0, y_last):
            x_sb = x_pool.tile([P, UNITS, C], BF16, tag="x")
            loads = []
            for b in range(IMAGES):
                pieces = [(0, P, 2 * b + wcol - 1, WS * wcol - CROP) for wcol in (1, 2)]
                pieces.append((0, LEFT, 4 + b, MAP - SEAM))
                pieces.append((LEFT, P, 4 + b, 0))
                for p0, p1, n, w0 in pieces:
                    w1_ = w0 + (p1 - p0) // ROWS
                    loads.append((x_sb[p0:p1, n, :], x_view[b, w0:w1_, y0 : y0 + ROWS, :]))
                    if y_last != y0 + ROWS - 1:
                        loads.append((x_sb[p0 + ROWS - 1 : p1 : ROWS, n, :], x_view[b, w0:w1_, y_last, :]))
            return x_sb, loads

        def load(to, source):
            nc.sync.dma_start(out=to, in_=source)

        vec_rows = act_pool.tile([P, K_PASS], BF16, tag="act")
        nc.vector.memset(vec_rows[:].bitcast(I32), 0)
        nc.sync.dma_start(out=vec_rows[0:PASSES, :], in_=g2.rearrange("(g c) -> g c", c=K_PASS))
        nc.sync.dma_start(out=vec_rows[PASSES : 2 * PASSES, :], in_=b2.rearrange("(g c) -> g c", c=K_PASS))
        sb_rows = act_pool.tile([P, 2 * P], BF16, tag="act")
        nc.vector.memset(sb_rows[:].bitcast(I32), 0)
        nc.sync.dma_start(out=sb_rows[0:HEADS, :], in_=sb)
        bias_rows = group_pool.tile([P, HID], BF16, tag="grouped", align_bytes=64)
        nc.vector.memset(bias_rows[:].bitcast(I32), 0)
        nc.sync.dma_start(out=bias_rows[0:1, :], in_=bb1.rearrange("(o n) -> o n", o=1))

        sw_nat = x1_pool.tile([P, 2, HEADS, WS * WS], BF16, tag="x1")
        for quad in range(HEADS // QUAD):
            hs = slice(QUAD * quad, QUAD * (quad + 1))
            nc.sync.dma_start(out=sw_nat[:, 0, hs], in_=sw_view[0][:, hs])
        windows, window_loads = load_windows(1)
        x_next, x_loads = load_x(WS - CROP, WS - CROP + ROWS - 1)
        for to, source in window_loads + x_loads:
            load(to, source)
        for quad in range(HEADS // QUAD):
            hs = slice(QUAD * quad, QUAD * (quad + 1))
            nc.sync.dma_start(out=sw_nat[:, 1, hs], in_=sw_view[1][:, hs])

        ident_f = const.tile([P, P], F32)
        make_identity(nc, ident_f[:])
        ident_b = const.tile([P, P], BF16)
        nc.vector.tensor_copy(out=ident_b[:], in_=ident_f[:])
        warm = small.tile([P, 2], F32, tag="warm")
        nc.scalar.activation(out=warm[:], in_=ident_f[:, 0:2], func=ACT.Gelu)
        by_columns = ident_f[:].rearrange("p (c r) -> p r c", c=WS, r=ROWS)
        by_rows = const.tile([P, ROWS, WS], F32)
        nc.vector.tensor_copy(out=by_rows[:], in_=by_columns)
        by_rows_seam = const.tile([P, ROWS, WS], F32)
        nc.vector.tensor_copy(out=by_rows_seam[:, :, SEAM:], in_=by_columns[:, :, SEAM:])
        nc.vector.tensor_copy(out=by_rows_seam[:, 1:, 0:SEAM], in_=by_columns[:, : ROWS - 1, 0:SEAM])
        nc.vector.tensor_copy(out=by_rows_seam[:, 0:1, 0:SEAM], in_=by_columns[:, ROWS - 1 :, 0:SEAM])
        to_tile = const.tile([P, WS, ROWS], BF16)
        nc.vector.tensor_copy(out=to_tile[:], in_=ident_f[:].rearrange("p (r c) -> p c r", c=WS, r=ROWS))
        minus_half = const.tile([P, 3], F32)
        nc.vector.memset(minus_half[:], -0.5)
        ones = act_pool.tile([P, P], BF16, tag="act")
        nc.vector.memset(ones[:], 1.0)

        whole = [const.tile([P, 2 * MARGIN + N_BLOCKS * P], BF16, name="whole%d" % half) for half in range(2)]
        split = [const.tile([P, 2 * MARGIN + N_BLOCKS * SPLIT], BF16, name="split%d" % half) for half in range(2)]
        orphan = const.tile([P, 2 * MARGIN + N_BLOCKS * P], BF16)
        orphan_split = const.tile([P, 2 * MARGIN + N_BLOCKS * SPLIT], BF16)

        def by_block(t, width):
            return t[:, MARGIN : MARGIN + N_BLOCKS * width].rearrange("p (n m) -> p n m", m=width)

        for t, width in ((whole[0], P), (split[0], SPLIT), (whole[1], P), (split[1], SPLIT)):
            nc.vector.memset(t[:, 0:MARGIN].bitcast(I32), 0)
            nc.vector.memset(t[:, MARGIN + N_BLOCKS * width :].bitcast(I32), 0)
            if width == SPLIT:
                nc.vector.memset(by_block(t, SPLIT)[:, :, LEFT : 2 * LEFT], 0.0)
        nc.gpsimd.memset(orphan[:].bitcast(I32), 0)
        nc.gpsimd.memset(orphan_split[:].bitcast(I32), 0)

        def prepare_quad(half, quad, copy):
            sw_ps = psum.tile([P, 2 * QUAD, P], BF16, tag="mix" if quad % 2 == 0 else "turn")
            for i in range(2 * QUAD):
                h, q = QUAD * quad + i // 2, i % 2
                nc.tensor.transpose(
                    out=sw_ps[:, i, :],
                    in_=sw_nat[:, half, h, :].rearrange("p (k q) -> p q k", q=2)[:, q, :],
                    identity=to_tile[:].rearrange("p c r -> p (c r)"),
                )
            ns = slice(2 * QUAD * quad, 2 * QUAD * (quad + 1))
            src = by_block(whole[half], P)[:, ns, :]
            dst = by_block(split[half], SPLIT)[:, ns, :]
            copy(out=src, in_=sw_ps[:])
            nc.vector.tensor_copy(out=dst[:, :, 0:LEFT], in_=src[:, :, 0:LEFT])
            nc.vector.tensor_copy(out=dst[:, :, 2 * LEFT :], in_=src[:, :, LEFT:])

        def first_rows(t, width, m0, m1):
            return by_block(t, width)[:, :, m0:m1].rearrange("p n (c r) -> p n c r", r=ROWS)[:, :, :, 0:1]

        def copy_row_8():
            nc.gpsimd.tensor_copy(out=first_rows(orphan, P, 0, P), in_=first_rows(whole[1], P, 0, P))
            nc.gpsimd.tensor_copy(out=first_rows(orphan_split, SPLIT, 0, LEFT), in_=first_rows(whole[1], P, 0, LEFT))
            nc.gpsimd.tensor_copy(
                out=first_rows(orphan_split, SPLIT, 2 * LEFT, SPLIT), in_=first_rows(whole[1], P, LEFT, P)
            )

        def clear_row_8():
            nc.gpsimd.memset(first_rows(whole[1], P, 0, P), 0.0)
            nc.gpsimd.memset(first_rows(split[1], SPLIT, 0, LEFT), 0.0)
            nc.gpsimd.memset(first_rows(split[1], SPLIT, 2 * LEFT, SPLIT), 0.0)

        w1_codes = const.tile([P, PASSES, HID], U32, align_bytes=64)
        w1_scales = const.tile([P, PASSES, HID], U8, align_bytes=64)
        w1_raw = {}

        def load_w1(g):
            w1_raw[g] = spare_pool.tile([P, PACK, HID], BF16, tag="spare", name="w1_raw")
            nc.sync.dma_start(out=w1_raw[g][:], in_=w1_view[g])

        def prepare_w1(g, half):
            ns = slice(HID // 2 * half, HID // 2 * (half + 1))
            grouped = group_pool.tile([P, HID // 2, PACK], BF16, tag="grouped", align_bytes=64)
            nc.vector.tensor_copy(out=grouped[:], in_=w1_raw[g][:, :, ns].rearrange("p t n -> p n t"))
            nc.vector.quantize_mx(
                out=w1_codes[:, g, ns].bitcast(FP8X4),
                scales=w1_scales[:, g, ns],
                in_=grouped[:].rearrange("p n t -> p (n t)"),
            )

        def accumulate(acc, terms):
            for i, (weights, moving) in enumerate(terms):
                nc.tensor.matmul(out=acc, lhsT=weights, rhs=moving, start=(i == 0), stop=(i == len(terms) - 1))

        def mix(sources, sb_index, x_sb, x1, h):
            cols = slice(HD * h, HD * (h + 1))
            inner_terms, seam_terms = [], []
            for (inner, last, first), whole_w, split_w, start in sources:
                for q in range(2):
                    n = 2 * h + q
                    w0 = MARGIN + P * n + start
                    s0 = MARGIN + SPLIT * n + start
                    inner_terms.append((whole_w[:, w0 : w0 + P], inner[:, :, q, cols]))
                    seam_terms.append((split_w[:, s0 : s0 + P], last[:, :, q, cols]))
                    seam_terms.append((split_w[:, s0 + LEFT : s0 + LEFT + P], first[:, :, q, cols]))
            acc = psum.tile([P, UNITS, HD], F32, tag="mix")
            accumulate(acc[:, 0:4, :], inner_terms)
            accumulate(acc[:, 4:6, :], seam_terms)
            nc.vector.scalar_tensor_tensor(
                out=x1[:, :, cols],
                in0=acc[:],
                scalar=sb_col[:, sb_index, h : h + 1],
                in1=x_sb[:, :, cols],
                op0=ALU.add,
                op1=ALU.add,
            )

        def units_of(b):
            return (4 + b, 2 * b, 2 * b + 1)

        def slots_of(st, b):
            x1 = st["x1"]
            if b == 0:
                return st["spare"][:], x1[:, 4, :], x1[:, 0, :]
            return x1[:, 1, :], x1[:, 5, :], x1[:, 2, :]

        def open_statistics(st, b, on_vector):
            st["on_vector", b] = on_vector
            st["mean_var", b] = small.tile([P, 3, 2], F32, tag="mean_var", name="mean_var")
            st["neg_mean", b] = small.tile([P, 3], F32, tag="neg_mean", name="neg_mean")
            st["squares", b] = small.tile([P, 3], F32, tag="squares", name="squares")
            st["rstd", b] = small.tile([P, 3], F32, tag="rstd", name="rstd")

        def moments(st, b, j):
            x1 = st["x1"][:, units_of(b)[j], :]
            stats = small.tile([P, 2, 6], F32, tag="stats")
            for i in range(2):
                nc.vector.bn_stats(out=stats[:, i, :], in_=x1[:, 512 * i : 512 * (i + 1)])
            nc.vector.bn_aggr(out=st["mean_var", b][:, j, :], in_=stats[:])

        def negative_mean(st, b, j):
            nc.scalar.activation(
                out=unread[:],
                in_=st["x1"][:, units_of(b)[j], :],
                func=ACT.Identity,
                scale=-1.0 / C,
                accum_out=st["neg_mean", b][:, j : j + 1],
            )

        def squared_distances(st, b, j):
            nc.scalar.activation(
                out=unread[:],
                in_=st["x1"][:, units_of(b)[j], :],
                func=ACT.Square,
                bias=st["neg_mean", b][:, j : j + 1],
                accum_out=st["squares", b][:, j : j + 1],
            )

        def inverse_deviation(st, b):
            nv, rstd = st["on_vector", b], st["rstd", b]
            if nv > 0:
                nc.gpsimd.tensor_scalar(
                    out=rstd[:, 0:nv],
                    in0=st["mean_var", b][:, 0:nv, 1],
                    scalar1=1.0,
                    scalar2=EPS,
                    op0=ALU.mult,
                    op1=ALU.add,
                )
            nc.gpsimd.tensor_scalar(
                out=rstd[:, nv:3],
                in0=st["squares", b][:, nv:3],
                scalar1=1.0 / C,
                scalar2=EPS,
                op0=ALU.mult,
                op1=ALU.add,
            )
            nc.gpsimd.tensor_tensor(out=rstd[:], in0=rstd[:], in1=minus_half[:], op=ALU.pow)

        def scale(st, b, j):
            if j < st["on_vector", b]:
                mean, op = st["mean_var", b][:, j, 0:1], ALU.subtract
            else:
                mean, op = st["neg_mean", b][:, j : j + 1], ALU.add
            nc.vector.tensor_scalar(
                out=slots_of(st, b)[j].rearrange("p (g t q) -> p g q t", g=PASSES, t=PACK),
                in0=st["x1"][:, units_of(b)[j], :].rearrange("p (g q t) -> p g q t", g=PASSES, t=PACK),
                scalar1=mean,
                scalar2=st["rstd", b][:, j : j + 1],
                op0=op,
                op1=ALU.mult,
            )

        def turn(st, b, k, on_vector):
            g, t = divmod(k, PACK)
            if t == 0:
                st["planes", b, g] = plane_pool.tile([P, PACK, STRIP], BF16, tag="planes", name="planes")
            turned = psum.tile([P, ROWS, MAP], F32, tag="turn")
            for i, y in enumerate(slots_of(st, b)):
                nc.tensor.transpose(
                    out=turned[:, :, WS * i : WS * (i + 1)],
                    in_=y[:, P * k : P * (k + 1)],
                    identity=by_rows_seam[:] if i == 0 else by_rows[:],
                )
            gain, shift = gain_shift[:, k : k + 1], gain_shift[:, BLOCKS + k : BLOCKS + k + 1]
            src, dst = turned[:].rearrange("p r w -> p (r w)"), st["planes", b, g][:, t, :]
            if on_vector:
                nc.vector.tensor_scalar(out=dst, in0=src, scalar1=gain, scalar2=shift, op0=ALU.mult, op1=ALU.add)
            else:
                nc.scalar.activation(out=dst, in_=src, func=ACT.Identity, scale=gain, bias=shift)

        def pack(st, b, g):
            st["grouped", b, g] = group_pool.tile([P, STRIP, PACK], BF16, tag="grouped", name="grouped", align_bytes=64)
            nc.vector.tensor_copy(
                out=st["grouped", b, g][:].rearrange("p (c i) t -> p c t i", i=4),
                in_=st["planes", b, g][:].rearrange("p t (c i) -> p c t i", i=4),
            )

        def quantise(st, b, g):
            if g == 0:
                st["codes", b] = code_pool.tile([P, PASSES, STRIP], U32, tag="codes", name="codes", align_bytes=64)
                st["scales", b] = code_pool.tile([P, PASSES, STRIP], U8, tag="scales", name="scales", align_bytes=64)
            for m0, m1 in ((0, 2 * P), (2 * P, 3 * P)):
                nc.vector.quantize_mx(
                    out=st["codes", b][:, g, m0:m1].bitcast(FP8X4),
                    scales=st["scales", b][:, g, m0:m1],
                    in_=st["grouped", b, g][:, m0:m1, :].rearrange("p a t -> p (a t)"),
                )

        def project(st, b, m):
            acc = psum_mx.tile([P, HID], F32, tag="mx", name="acc")
            for g in range(PASSES):
                nc.tensor.matmul_mx(
                    out=acc[:],
                    lhsT=st["codes", b][:, g, P * m : P * (m + 1)].bitcast(FP8X4),
                    lhsT_scale=st["scales", b][:, g, P * m : P * (m + 1)],
                    rhs=w1_codes[:, g, :].bitcast(FP8X4),
                    rhs_scale=w1_scales[:, g, :],
                    start=(g == 0),
                    stop=(g == PASSES - 1),
                )
            st["acc", b, m] = acc

        def finish(st, b, m):
            act = act_pool.tile([P, HID], F32, tag="act")
            nc.vector.tensor_tensor(out=act[:], in0=st["acc", b, m][:], in1=bias_bc[:], op=ALU.add)
            nc.scalar.activation(out=act[:], in_=act[:], func=ACT.Gelu)
            y0, y_last = st["rows"]
            pieces = []
            if m == 0:
                pieces.append((0, SEAM, y_last * MAP + MAP - SEAM))
            p0, p1 = max(P * m, SEAM), P * (m + 1)
            cut = min(max(SEAM + STRIP - MAP, p0), p1)
            pieces.append((p0, cut, y0 * MAP + p0 - SEAM))
            pieces.append((cut, p1, y_last * MAP + cut - SEAM - (STRIP - MAP)))
            for s0, s1, row in pieces:
                mid = s0 + (s1 - s0) // 16 * 16
                for a, z in ((s0, mid), (mid, s1)):
                    if a < z:
                        nc.sync.dma_start(
                            out=out[b, row + a - s0 : row + z - s0, :], in_=act[a - P * m : z - P * m, :]
                        )

        vec_perm = plane_pool.tile([P, PACK, P], BF16, tag="planes")
        nc.vector.tensor_copy(out=vec_perm[:], in_=vec_rows[:].rearrange("p (q t) -> p t q", t=PACK))
        sb_perm = plane_pool.tile([P, 3, WS, ROWS], BF16, tag="planes")
        nc.vector.tensor_copy(
            out=sb_perm[:, 0:2, :, :], in_=sb_rows[:].rearrange("p (t r c) -> p t c r", t=2, r=ROWS, c=WS)
        )
        nc.vector.tensor_copy(out=sb_perm[:, 2, :, 0 : ROWS - 1], in_=sb_perm[:, 1, :, 1:ROWS])
        nc.vector.tensor_copy(out=sb_perm[:, 2, :, ROWS - 1 : ROWS], in_=sb_perm[:, 1, :, 0:1])
        vec_ps = psum_mx.tile([P, PACK + 3, P], BF16, tag="mx")
        for t in range(PACK):
            nc.tensor.transpose(out=vec_ps[:, t, :], in_=vec_perm[:, t, :], identity=ident_b[:])
        for i in range(3):
            nc.tensor.transpose(
                out=vec_ps[:, PACK + i, :], in_=sb_perm[:, i, :, :].rearrange("p c r -> p (c r)"), identity=ident_b[:]
            )
        gain_shift = const.tile([P, 2 * BLOCKS], F32)
        nc.vector.tensor_copy(
            out=gain_shift[:].rearrange("p (r t) -> p r t", t=PACK),
            in_=vec_ps[:, 0:PACK, 0 : 2 * PASSES].rearrange("p t r -> p r t"),
        )
        sb_col = const.tile([P, 3, HEADS], F32)
        nc.vector.tensor_copy(out=sb_col[:], in_=vec_ps[:, PACK : PACK + 3, 0:HEADS])
        bias_ps = psum_mx.tile([P, HID], F32, tag="mx")
        nc.tensor.matmul(out=bias_ps[:], lhsT=ones[:], rhs=bias_rows[:], start=True, stop=True)
        bias_bc = const.tile([P, HID], BF16)
        nc.vector.tensor_copy(out=bias_bc[:], in_=bias_ps[:])
        for quad in range(HEADS // QUAD):
            prepare_quad(0, quad, nc.vector.tensor_copy if quad % 2 == 0 else nc.scalar.copy)
        unread = const.tile([P, C], BF16)

        stages = []
        for wrow in (1, 2, 3):
            for half in range(2):
                y0 = WS * wrow + ROWS * half - CROP
                if y0 + ROWS <= MAP:
                    stages.append(((wrow,), half, y0, y0 + ROWS - 1))
        stages.append(((0, WINDOWS - 1), 2, 0, MAP - 1))
        n_stages = len(stages)
        last_second_half = max(i for i, stage in enumerate(stages) if stage[1] == 1)

        def live(i):
            return 0 <= i < n_stages

        held = {1: windows}

        def sources_of(i):
            wrows, half = stages[i][0], stages[i][1]
            if half < 2:
                return [(held[wrows[0]], whole[half], split[half], 0)]
            return [(held[wrows[0]], whole[1], split[1], 1), (held[wrows[1]], orphan, orphan_split, 1 - ROWS)]

        fetch_round = {2: 0, 3: 2, 0: 4}

        def older_work(ripe, late):
            at = [[] for i in range(HEADS)]
            if late is not None:
                at[0].append((finish, late, 0, 1))
                at[0].append((pack, late, 1, 0))
                at[1].append((finish, late, 0, 2))
            if ripe is not None:
                alone = ripe is states.get(n_stages - 1)
                open_statistics(ripe, 0, 1)
                open_statistics(ripe, 1, 2 if alone else 0)
                for b in range(IMAGES):
                    for j in range(ripe["on_vector", b]):
                        at[b + j].append((moments, ripe, b, j))
                for j in (1, 2):
                    at[0].append((negative_mean, ripe, 0, j))
                for j in (1, 2):
                    at[1].append((squared_distances, ripe, 0, j))
                at[2].append((inverse_deviation, ripe, 0))
                scalar_tiles = range(ripe["on_vector", 1], 3)
                for i, j in enumerate(scalar_tiles):
                    at[3 + i].append((negative_mean, ripe, 1, j))
                for i, j in enumerate(scalar_tiles):
                    at[7 + i].append((squared_distances, ripe, 1, j))
                at[4].append((scale, ripe, 0, 0))
                at[5].append((scale, ripe, 0, 1))
                at[5].append((scale, ripe, 0, 2))
                for k in range(BLOCKS):
                    at[6 + k // 2].append((turn, ripe, 0, k, alone and k % 2 == 1))
                at[9].append((pack, ripe, 0, 0))
                at[10].append((inverse_deviation, ripe, 1))
                at[10].append((pack, ripe, 0, 1))
                at[11].append((scale, ripe, 1, 0))
                at[11].append((scale, ripe, 1, 1))
                at[12].append((scale, ripe, 1, 2))
                at[12].append((quantise, ripe, 0, 0))
                at[13].append((quantise, ripe, 0, 1))
                for k in range(BLOCKS):
                    at[13 + k // 3].append((turn, ripe, 1, k, alone and k % 2 == 1))
                for m in range(STRIP_TILES):
                    at[(14, 15, 15)[m]].append((project, ripe, 0, m))
                at[15].append((finish, ripe, 0, 0))
            if late is not None:
                at[1].append((pack, late, 1, 1))
                at[2].append((quantise, late, 1, 0))
                at[3].append((quantise, late, 1, 1))
                for m in range(STRIP_TILES):
                    at[4 + m].append((project, late, 1, m))
                    at[5 + m].append((finish, late, 1, m))
            return at

        states = {}
        x_of = {0: x_next}
        with tc.manual_schedule(engines={mybir.EngineType.SP}):
            for fresh in range(n_stages + 2):
                if live(fresh):
                    states[fresh] = {
                        "x1": x1_pool.tile([P, UNITS, C], F32, tag="x1", name="x1"),
                        "rows": stages[fresh][2:],
                    }
                if live(fresh - 1):
                    states[fresh - 1]["spare"] = spare_pool.tile([P, C], F32, tag="spare", name="spare")
                at = older_work(states.get(fresh - 1) if live(fresh - 1) else None, states.get(fresh - 2) if live(fresh - 2) else None)
                if live(fresh + 1):
                    x_of[fresh + 1], loads = load_x(stages[fresh + 1][2], stages[fresh + 1][3])
                    for i, (to, source) in enumerate(loads):
                        at[i * HEADS // len(loads)].append((load, to, source))
                for wrow, fetched in fetch_round.items():
                    if fetched == fresh:
                        held[wrow], loads = load_windows(wrow)
                        for i, (to, source) in enumerate(loads):
                            at[2 * i].append((load, to, source))
                if fresh == 0:
                    load_w1(0)
                    for quad in range(HEADS // QUAD):
                        at[3 + 2 * quad].append((prepare_quad, 1, quad, nc.scalar.copy))
                    at[10].append((prepare_w1, 0, 0))
                    at[11].append((prepare_w1, 0, 1))
                    at[11].append((load_w1, 1))
                    at[14].append((prepare_w1, 1, 0))
                    at[15].append((prepare_w1, 1, 1))
                if fresh == 1:
                    at[15].append((copy_row_8,))
                if fresh == last_second_half + 1:
                    at[11].append((clear_row_8,))
                for h in range(HEADS):
                    if live(fresh):
                        mix(sources_of(fresh), stages[fresh][1], x_of[fresh], states[fresh]["x1"], h)
                    for call in at[h]:
                        call[0](*call[1:])
